import numpy as np
import ml_dtypes


def mxq(x, axis, fmt="e4m3"):
    dtype, down = {"e4m3": (ml_dtypes.float8_e4m3fn, 7), "e5m2": (ml_dtypes.float8_e5m2, 14)}[fmt]
    v = np.moveaxis(np.asarray(x, np.float32).astype(ml_dtypes.bfloat16).astype(np.float64), axis, -1)
    blocks = v.reshape(v.shape[:-1] + (-1, 32))
    amax = np.abs(blocks).max(-1, keepdims=True)
    byte = np.maximum(np.where(amax > 0, np.frexp(amax)[1] - 1 + 127, 0) - down, 1)
    scale = np.exp2(byte - 127.0)
    codes = (blocks / scale).astype(np.float32).astype(dtype).astype(np.float64)
    return np.moveaxis((codes * scale).reshape(v.shape), -1, axis)


WIDE = False


def mx_kscale(k):
    if not WIDE:
        return np.ones(k)
    levels = np.array([10, -10, 5, -5, 0])
    a = np.random.permutation(np.resize(levels, k // 512 * 4)).reshape(k // 512, 4)
    idx = np.arange(k)
    return np.exp2(a[idx // 512, idx % 128 // 32])


BF16 = ml_dtypes.bfloat16


def bf(x):
    return np.asarray(x, np.float32).astype(BF16)


def f64(x):
    return np.asarray(x).astype(np.float64)


B, S, D, H, HD, P = 2, 256, 2048, 16, 128, 512
K = H * HD
P_RMS = 2.0
A_RMS = np.sqrt(np.e * np.log(S) / S)


def setup_inputs():
    t = mx_kscale(K).reshape(H, HD)
    return {"q_rot": bf(np.random.standard_normal((B, H, S, HD))),
            "pk": bf(np.random.standard_normal((P, H, HD)) * P_RMS),
            "pv": bf(np.abs(np.random.standard_normal((P, H, HD))) * P_RMS * t[None, :, :]),
            "prompt_gate": bf(np.random.uniform(0.25, 0.75, (1, H, 1, 1))),
            "h_attn": bf(np.abs(np.random.standard_normal((B, H, S, HD))) * A_RMS * t[None, :, None, :]),
            "wo": bf(np.random.standard_normal((D, K)) / np.sqrt(K) / t.reshape(-1)[None, :])}


def reference(q_rot, pk, pv, prompt_gate, h_attn, wo):
    ps = f64(q_rot) @ f64(pk).transpose(1, 2, 0) * (1.0 / np.sqrt(HD))
    e = np.exp(ps - ps.max(-1, keepdims=True))
    num = mxq(e, 3, "e4m3") @ mxq(f64(pv).transpose(1, 0, 2), 1, "e4m3")
    p_out = f64(prompt_gate) * num / e.sum(-1, keepdims=True)
    fused = (f64(h_attn) + p_out).transpose(0, 2, 1, 3).reshape(B, S, K)
    return mxq(fused, 2, "e4m3") @ mxq(f64(wo), 1, "e4m3").T

@@ -1,0 +1,346 @@
+import math
+from contextlib import ExitStack
+
+import concourse.mybir as mybir
+from concourse.masks import make_identity
+
+F32 = mybir.dt.float32
+BF16 = mybir.dt.bfloat16
+U32 = mybir.dt.uint32
+U8 = mybir.dt.uint8
+FP8X4 = mybir.dt.float8_e4m3fn_x4
+ACT = mybir.ActivationFunctionType
+ALU = mybir.AluOpType
+AXIS = mybir.AxisListType
+
+P = 128
+BATCH, HEADS, SEQ, HEAD_DIM, PROMPT, D_OUT = 2, 16, 256, 128, 512, 2048
+K_FUSED = HEADS * HEAD_DIM
+K_PASS = 4 * P
+PASSES = K_FUSED // K_PASS
+GROUP = K_PASS // HEAD_DIM
+ROW_TILES = BATCH * SEQ // P
+N_TILE = 512
+WO_CHUNK = 2 * P
+WO_CHUNKS = D_OUT // WO_CHUNK
+SCALE = 1.0 / math.sqrt(HEAD_DIM)
+
+FLOPS = 2 * (2 * BATCH * HEADS * SEQ * HEAD_DIM * PROMPT) + 2 * BATCH * SEQ * K_FUSED * D_OUT
+
+
+def tile_attention_pb_kernel(tc, q_rot, pk, pv, prompt_gate, h_attn, wo, out):
+    nc = tc.nc
+
+    q_view = q_rot.rearrange("b h (m t) d -> b m h (t d)", t=2)
+    ha_view = h_attn.rearrange("b h (m t) d -> b m h (t d)", t=2)
+    out_view = out.rearrange("b (m t) n -> b t m n", t=2)
+    pk_view = pk.rearrange("(c p) h d -> p c (h d)", p=P)
+    pv_view = pv.rearrange("(u q e) h d -> u q e (h d)", u=2, e=2)
+    wo_view = wo.rearrange("(n p) k -> p n k", p=P)
+
+    with ExitStack() as ctx:
+        keep = ctx.enter_context(tc.tile_pool(name="keep", bufs=1))
+        raw = ctx.enter_context(tc.tile_pool(name="raw", bufs=3))
+        work = ctx.enter_context(tc.tile_pool(name="work", bufs=3))
+        e_pool = ctx.enter_context(tc.tile_pool(name="e_pool", bufs=10))
+        stats = ctx.enter_context(tc.tile_pool(name="stats", bufs=6))
+        results = ctx.enter_context(tc.tile_pool(name="results", bufs=4))
+        psum_ps = ctx.enter_context(tc.psum_pool(name="psum_ps", bufs=3))
+        psum_tr = ctx.enter_context(tc.psum_pool(name="psum_tr", bufs=4))
+        psum_num = ctx.enter_context(tc.psum_pool(name="psum_num", bufs=1))
+        ctx.enter_context(tc.manual_schedule())
+
+        ident_bf = keep.tile([P, P], BF16)
+        make_identity(nc, ident_bf[:])
+        ident_f32 = keep.tile([P, P], F32)
+        make_identity(nc, ident_f32[:])
+
+        q_sb = keep.tile([P, BATCH, HEADS, 2 * HEAD_DIM], BF16)
+        ha_sb = keep.tile([P, BATCH, HEADS, 2 * HEAD_DIM], BF16)
+        pkT = keep.tile([P, HEADS, PROMPT], BF16)
+        pv_codes = keep.tile([P, K_FUSED], U32, align_bytes=64)
+        pv_scales = keep.tile([P, K_FUSED], U8, align_bytes=64)
+        wo_codes = keep.tile([P, PASSES, D_OUT], U32, align_bytes=64)
+        wo_scales = keep.tile([P, PASSES, D_OUT], U8, align_bytes=64)
+        fused_codes = keep.tile([P, ROW_TILES, PASSES, P], U32, align_bytes=64)
+        fused_scales = keep.tile([P, ROW_TILES, PASSES, P], U8, align_bytes=64)
+
+        gate_bf = keep.tile([P, HEADS], BF16)
+        nc.sync.dma_start(
+            out=gate_bf[:], in_=prompt_gate.rearrange("a h b c -> (a h b c)").partition_broadcast(P)
+        )
+        gate = keep.tile([P, HEADS], F32)
+        nc.vector.tensor_copy(out=gate[:], in_=gate_bf[:])
+
+        pk_raw, pv_raw, wo_raw, pv_grouped, wo_grouped = {}, {}, {}, {}, {}
+        qT, top, shift, rowsum, weight = {}, {}, {}, {}, {}
+        e_sb, e_grouped, e_codes, e_scales, num_ps, fused, f_grouped, acc = {}, {}, {}, {}, {}, {}, {}, {}
+
+        def load_queries(b, g):
+            heads = slice(GROUP * g, GROUP * (g + 1))
+            nc.sync.dma_start(out=q_sb[:, b, heads, :], in_=q_view[b][:, heads, :])
+            nc.sync.dma_start(out=ha_sb[:, b, heads, :], in_=ha_view[b][:, heads, :])
+
+        def load_prompt(g):
+            cols = slice(K_PASS * g, K_PASS * (g + 1))
+            pk_raw[g] = raw.tile([P, PROMPT // P, K_PASS], BF16, tag="pk_raw", name="pk_raw")
+            nc.sync.dma_start(out=pk_raw[g][:], in_=pk_view[:, :, cols])
+            pv_raw[g] = raw.tile([P, 4, K_PASS], BF16, tag="pv_raw", name="pv_raw")
+            for u in range(2):
+                nc.sync.dma_start(out=pv_raw[g][:, 2 * u : 2 * u + 2, :], in_=pv_view[u][:, :, cols])
+
+        def load_wo(chunk):
+            wo_raw[chunk] = raw.tile([P, WO_CHUNK // P, K_FUSED], BF16, tag="wo_raw", name="wo_raw")
+            nc.sync.dma_start(out=wo_raw[chunk][:], in_=wo_view[:, 2 * chunk : 2 * chunk + 2, :])
+
+        def flip_keys(h):
+            g, i = divmod(h, GROUP)
+            pkT_ps = psum_tr.tile([P, PROMPT // P, P], BF16, tag="tr")
+            for c in range(PROMPT // P):
+                nc.tensor.transpose(
+                    pkT_ps[:, c, :], pk_raw[g][:, c, HEAD_DIM * i : HEAD_DIM * (i + 1)], ident_bf[:]
+                )
+            nc.scalar.copy(out=pkT[:, h, :], in_=pkT_ps[:].rearrange("d c p -> d (c p)"))
+
+        def group_values(g):
+            pv_grouped[g] = work.tile([P, K_PASS, 4], BF16, tag="pv_grouped", name="pv_grouped", align_bytes=64)
+            nc.vector.tensor_copy(out=pv_grouped[g][:], in_=pv_raw[g][:].rearrange("q j c -> q c j"))
+
+        def quantise_values(g):
+            cols = slice(K_PASS * g, K_PASS * (g + 1))
+            nc.vector.quantize_mx(
+                out=pv_codes[:, cols].bitcast(FP8X4),
+                scales=pv_scales[:, cols],
+                in_=pv_grouped[g][:].rearrange("q c j -> q (c j)"),
+            )
+
+        def flip_wo(unit):
+            chunk, g = divmod(unit, PASSES)
+            woT_ps = psum_tr.tile([P, 2, 2, P], F32, tag="tr")
+            for n in range(2):
+                words = wo_raw[chunk][:, n, :].bitcast(F32)
+                for u in range(2):
+                    first = (K_PASS * g + 2 * P * u) // 2
+                    nc.tensor.transpose(woT_ps[:, n, u, :], words[:, first : first + P], ident_f32[:])
+            wo_grouped[unit] = work.tile([P, 4 * WO_CHUNK], BF16, tag="wo_grouped", name="wo_grouped", align_bytes=64)
+            nc.scalar.copy(
+                out=wo_grouped[unit][:].bitcast(F32).rearrange("q (n p u) -> q n p u", n=2, u=2),
+                in_=woT_ps[:].rearrange("q n u p -> q n p u"),
+            )
+
+        def quantise_wo(unit):
+            chunk, g = divmod(unit, PASSES)
+            cols = slice(WO_CHUNK * chunk, WO_CHUNK * (chunk + 1))
+            nc.vector.quantize_mx(
+                out=wo_codes[:, g, cols].bitcast(FP8X4), scales=wo_scales[:, g, cols], in_=wo_grouped[unit][:]
+            )
+
+        def flip_queries(r):
+            rt, g = divmod(r, PASSES)
+            b, t = divmod(rt, 2)
+            qT_ps = psum_tr.tile([P, GROUP, P], BF16, tag="tr")
+            for j in range(GROUP):
+                nc.tensor.transpose(
+                    qT_ps[:, j, :], q_sb[:, b, GROUP * g + j, HEAD_DIM * t : HEAD_DIM * (t + 1)], ident_bf[:]
+                )
+            qT[r] = stats.tile([P, GROUP, P], BF16, tag="qT", name="qT")
+            nc.scalar.copy(out=qT[r][:], in_=qT_ps[:])
+            top[r] = stats.tile([P, GROUP], F32, tag="top", name="top")
+            shift[r] = stats.tile([P, GROUP], F32, tag="shift", name="shift")
+            rowsum[r] = stats.tile([P, GROUP], F32, tag="rowsum", name="rowsum")
+
+        def score(i):
+            r, j = divmod(i, GROUP)
+            one = slice(j, j + 1)
+            ps = psum_ps.tile([P, PROMPT], F32, tag="ps")
+            nc.tensor.matmul(ps[:], lhsT=qT[r][:, j, :], rhs=pkT[:, i % HEADS, :], start=True, stop=True)
+            nc.vector.reduce_max(out=top[r][:, one], in_=ps[:], axis=AXIS.X)
+            nc.vector.tensor_scalar_mul(out=shift[r][:, one], in0=top[r][:, one], scalar1=-SCALE)
+            e_sb[i] = e_pool.tile([P, PROMPT], BF16, tag="e_sb", name="e_sb")
+            nc.scalar.activation(
+                out=e_sb[i][:],
+                in_=ps[:],
+                func=ACT.Exp,
+                bias=shift[r][:, one],
+                scale=SCALE,
+                accum_out=rowsum[r][:, one],
+            )
+
+        def flip_e(pair):
+            r, half = divmod(pair, 2)
+            if half == 0:
+                e_grouped[r] = work.tile([P, GROUP * P * 4], BF16, tag="e_grouped", name="e_grouped", align_bytes=64)
+            eT_ps = psum_tr.tile([P, 2, 2, P], F32, tag="tr")
+            for j in range(2):
+                words = e_sb[2 * pair + j][:].bitcast(F32)
+                for u in range(2):
+                    nc.tensor.transpose(eT_ps[:, j, u, :], words[:, P * u : P * (u + 1)], ident_f32[:])
+            e_words = e_grouped[r][:].bitcast(F32).rearrange("q (j m u) -> q j m u", j=GROUP, u=2)
+            nc.scalar.copy(
+                out=e_words[:, 2 * half : 2 * half + 2, :, :], in_=eT_ps[:].rearrange("q j u m -> q j m u")
+            )
+
+        def quantise_e(r):
+            g = r % PASSES
+            e_codes[r] = work.tile([P, GROUP * P], U32, tag="e_codes", name="e_codes", align_bytes=64)
+            e_scales[r] = work.tile([P, GROUP * P], U8, tag="e_scales", name="e_scales", align_bytes=64)
+            nc.vector.quantize_mx(
+                out=e_codes[r][:].bitcast(FP8X4), scales=e_scales[r][:], in_=e_grouped[r][:]
+            )
+            weight[r] = stats.tile([P, GROUP], F32, tag="weight", name="weight")
+            nc.vector.reciprocal(out=weight[r][:], in_=rowsum[r][:])
+            nc.vector.tensor_mul(
+                out=weight[r][:], in0=weight[r][:], in1=gate[:, GROUP * g : GROUP * (g + 1)]
+            )
+
+        def multiply_values(r):
+            g = r % PASSES
+            num_ps[r] = psum_num.tile([P, GROUP, HEAD_DIM], F32, tag="num", name="num_ps")
+            for j in range(GROUP):
+                e_cols = slice(P * j, P * (j + 1))
+                v_cols = slice(HEAD_DIM * (GROUP * g + j), HEAD_DIM * (GROUP * g + j + 1))
+                nc.tensor.matmul_mx(
+                    out=num_ps[r][:, j, :],
+                    lhsT=e_codes[r][:, e_cols].bitcast(FP8X4),
+                    lhsT_scale=e_scales[r][:, e_cols],
+                    rhs=pv_codes[:, v_cols].bitcast(FP8X4),
+                    rhs_scale=pv_scales[:, v_cols],
+                    start=True,
+                    stop=True,
+                )
+
+        def combine(r, half):
+            rt, g = divmod(r, PASSES)
+            b, t = divmod(rt, 2)
+            if half == 0:
+                fused[r] = work.tile([P, K_PASS], BF16, tag="fused", name="fused")
+            for j in range(2 * half, 2 * half + 2):
+                nc.vector.scalar_tensor_tensor(
+                    out=fused[r][:, HEAD_DIM * j : HEAD_DIM * (j + 1)],
+                    in0=num_ps[r][:, j, :],
+                    scalar=weight[r][:, j : j + 1],
+                    in1=ha_sb[:, b, GROUP * g + j, HEAD_DIM * t : HEAD_DIM * (t + 1)],
+                    op0=ALU.mult,
+                    op1=ALU.add,
+                )
+
+        def flip_fused(r):
+            fT_ps = psum_tr.tile([P, 2, P], F32, tag="tr")
+            for u in range(2):
+                nc.tensor.transpose(
+                    fT_ps[:, u, :], fused[r][:].bitcast(F32)[:, P * u : P * (u + 1)], ident_f32[:]
+                )
+            f_grouped[r] = work.tile([P, P * 4], BF16, tag="f_grouped", name="f_grouped", align_bytes=64)
+            nc.scalar.copy(
+                out=f_grouped[r][:].bitcast(F32).rearrange("q (m u) -> q m u", u=2),
+                in_=fT_ps[:].rearrange("q u m -> q m u"),
+            )
+
+        def quantise_fused(r):
+            rt, g = divmod(r, PASSES)
+            nc.vector.quantize_mx(
+                out=fused_codes[:, rt, g, :].bitcast(FP8X4),
+                scales=fused_scales[:, rt, g, :],
+                in_=f_grouped[r][:],
+            )
+
+        def project(piece):
+            rt, n = divmod(piece, D_OUT // N_TILE)
+            cols = slice(N_TILE * n, N_TILE * (n + 1))
+            acc[piece] = psum_tr.tile([P, N_TILE], F32, tag="tr", name="acc")
+            for g in range(PASSES):
+                nc.tensor.matmul_mx(
+                    out=acc[piece][:],
+                    lhsT=fused_codes[:, rt, g, :].bitcast(FP8X4),
+                    lhsT_scale=fused_scales[:, rt, g, :],
+                    rhs=wo_codes[:, g, cols].bitcast(FP8X4),
+                    rhs_scale=wo_scales[:, g, cols],
+                    start=(g == 0),
+                    stop=(g == PASSES - 1),
+                )
+
+        def store(piece):
+            rt, n = divmod(piece, D_OUT // N_TILE)
+            b, t = divmod(rt, 2)
+            result = results.tile([P, N_TILE], F32, tag="result")
+            if piece % 2 == 0:
+                nc.scalar.copy(out=result[:], in_=acc[piece][:])
+            else:
+                nc.vector.tensor_copy(out=result[:], in_=acc[piece][:])
+            nc.sync.dma_start(out=out_view[b, t][:, N_TILE * n : N_TILE * (n + 1)], in_=result[:])
+
+        def due(i, first, every, count):
+            k, rest = divmod(i - first, every)
+            return k if rest == 0 and 0 <= k < count else None
+
+        steps = ROW_TILES * HEADS
+        rounds = steps // GROUP
+        units = WO_CHUNKS * PASSES
+        n_tiles = D_OUT // N_TILE
+
+        for g in range(2):
+            load_prompt(g)
+            load_queries(0, g)
+            load_wo(g)
+        flip_keys(0)
+        flip_keys(1)
+        flip_queries(0)
+
+        for i in range(steps + 28):
+            ahead = due(i, -8, 4, WO_CHUNKS)
+            if ahead is not None and ahead >= 2:
+                if ahead < PASSES:
+                    load_prompt(ahead)
+                    load_queries(0, ahead)
+                load_wo(ahead)
+                if PASSES <= ahead < PASSES + 2:
+                    load_queries(1, 2 * (ahead - PASSES))
+                    load_queries(1, 2 * (ahead - PASSES) + 1)
+
+            r_values = due(i, 11, 4, rounds)
+            if r_values is not None:
+                multiply_values(r_values)
+            rt_piece, rest = divmod(i - 34, HEADS)
+            n_piece = due(rest, 0, 3, n_tiles)
+            piece = None
+            if 0 <= rt_piece < ROW_TILES and n_piece is not None:
+                piece = n_tiles * rt_piece + n_piece
+                project(piece)
+            if i < steps:
+                score(i)
+            pair = due(i, 5, 2, steps // 2)
+            if pair is not None:
+                flip_e(pair)
+            r_fused = due(i, 16, 4, rounds)
+            if r_fused is not None:
+                flip_fused(r_fused)
+            r_next = due(i, -4, 4, rounds)
+            if r_next is not None and r_next >= 1:
+                flip_queries(r_next)
+            if i + 2 < HEADS:
+                flip_keys(i + 2)
+            unit = due(i, 0, 1, units)
+            if unit is not None:
+                flip_wo(unit)
+
+            for half in range(2):
+                r_comb = due(i, 11 + half, 4, rounds)
+                if r_comb is not None:
+                    combine(r_comb, half)
+            r_e = due(i, 8, 4, rounds)
+            if r_e is not None:
+                quantise_e(r_e)
+            r_q = due(i, 18, 4, rounds)
+            if r_q is not None:
+                quantise_fused(r_q)
+            unit = due(i, 0 + 1, 1, units)
+            if unit is not None:
+                quantise_wo(unit)
+            g_group = due(i, 2, 4, PASSES)
+            if g_group is not None:
+                group_values(g_group)
+            g_quant = due(i, 4, 4, PASSES)
+            if g_quant is not None:
+                quantise_values(g_quant)
+            if piece is not None:
+                store(piece)

@@ -11,7 +11,6 @@ U8 = mybir.dt.uint8
 FP8X4 = mybir.dt.float8_e4m3fn_x4
 ACT = mybir.ActivationFunctionType
 ALU = mybir.AluOpType
-AXIS = mybir.AxisListType
 
 P = 128
 BATCH, HEADS, SEQ, HEAD_DIM, PROMPT, D_OUT = 2, 16, 256, 128, 512, 2048
@@ -42,13 +41,14 @@ def tile_attention_pb_kernel(tc, q_rot, pk, pv, prompt_gate, h_attn, wo, out):
         keep = ctx.enter_context(tc.tile_pool(name="keep", bufs=1))
         raw = ctx.enter_context(tc.tile_pool(name="raw", bufs=3))
         work = ctx.enter_context(tc.tile_pool(name="work", bufs=3))
-        e_pool = ctx.enter_context(tc.tile_pool(name="e_pool", bufs=10))
+        e_pool = ctx.enter_context(tc.tile_pool(name="e_pool", bufs=8))
         stats = ctx.enter_context(tc.tile_pool(name="stats", bufs=6))
+        s_pool = ctx.enter_context(tc.tile_pool(name="s_pool", bufs=4))
         results = ctx.enter_context(tc.tile_pool(name="results", bufs=4))
-        psum_ps = ctx.enter_context(tc.psum_pool(name="psum_ps", bufs=3))
+        psum_ps = ctx.enter_context(tc.psum_pool(name="psum_ps", bufs=2))
         psum_tr = ctx.enter_context(tc.psum_pool(name="psum_tr", bufs=4))
         psum_num = ctx.enter_context(tc.psum_pool(name="psum_num", bufs=1))
-        ctx.enter_context(tc.manual_schedule())
+        psum_acc = ctx.enter_context(tc.psum_pool(name="psum_acc", bufs=1))
 
         ident_bf = keep.tile([P, P], BF16)
         make_identity(nc, ident_bf[:])
@@ -73,7 +73,7 @@ def tile_attention_pb_kernel(tc, q_rot, pk, pv, prompt_gate, h_attn, wo, out):
         nc.vector.tensor_copy(out=gate[:], in_=gate_bf[:])
 
         pk_raw, pv_raw, wo_raw, pv_grouped, wo_grouped = {}, {}, {}, {}, {}
-        qT, top, shift, rowsum, weight = {}, {}, {}, {}, {}
+        qT, scaled, shift, rowsum, weight = {}, {}, {}, {}, {}
         e_sb, e_grouped, e_codes, e_scales, num_ps, fused, f_grouped, acc = {}, {}, {}, {}, {}, {}, {}, {}
 
         def load_queries(b, g):
@@ -100,10 +100,10 @@ def tile_attention_pb_kernel(tc, q_rot, pk, pv, prompt_gate, h_attn, wo, out):
                 nc.tensor.transpose(
                     pkT_ps[:, c, :], pk_raw[g][:, c, HEAD_DIM * i : HEAD_DIM * (i + 1)], ident_bf[:]
                 )
-            nc.scalar.copy(out=pkT[:, h, :], in_=pkT_ps[:].rearrange("d c p -> d (c p)"))
+            nc.vector.tensor_copy(out=pkT[:, h, :], in_=pkT_ps[:].rearrange("d c p -> d (c p)"))
 
         def group_values(g):
-            pv_grouped[g] = work.tile([P, K_PASS, 4], BF16, tag="pv_grouped", name="pv_grouped", align_bytes=64)
+            pv_grouped[g] = work.tile([P, K_PASS, 4], BF16, tag="pv_grouped", name="pv_grouped", bufs=2, align_bytes=64)
             nc.vector.tensor_copy(out=pv_grouped[g][:], in_=pv_raw[g][:].rearrange("q j c -> q c j"))
 
         def quantise_values(g):
@@ -144,8 +144,7 @@ def tile_attention_pb_kernel(tc, q_rot, pk, pv, prompt_gate, h_attn, wo, out):
                     qT_ps[:, j, :], q_sb[:, b, GROUP * g + j, HEAD_DIM * t : HEAD_DIM * (t + 1)], ident_bf[:]
                 )
             qT[r] = stats.tile([P, GROUP, P], BF16, tag="qT", name="qT")
-            nc.scalar.copy(out=qT[r][:], in_=qT_ps[:])
-            top[r] = stats.tile([P, GROUP], F32, tag="top", name="top")
+            nc.vector.tensor_copy(out=qT[r][:], in_=qT_ps[:])
             shift[r] = stats.tile([P, GROUP], F32, tag="shift", name="shift")
             rowsum[r] = stats.tile([P, GROUP], F32, tag="rowsum", name="rowsum")
 
@@ -154,15 +153,23 @@ def tile_attention_pb_kernel(tc, q_rot, pk, pv, prompt_gate, h_attn, wo, out):
             one = slice(j, j + 1)
             ps = psum_ps.tile([P, PROMPT], F32, tag="ps")
             nc.tensor.matmul(ps[:], lhsT=qT[r][:, j, :], rhs=pkT[:, i % HEADS, :], start=True, stop=True)
-            nc.vector.reduce_max(out=top[r][:, one], in_=ps[:], axis=AXIS.X)
-            nc.vector.tensor_scalar_mul(out=shift[r][:, one], in0=top[r][:, one], scalar1=-SCALE)
+            scaled[i] = s_pool.tile([P, PROMPT], F32, tag="scaled", name="scaled")
+            nc.vector.tensor_scalar(
+                out=scaled[i][:],
+                in0=ps[:],
+                scalar1=-SCALE,
+                scalar2=None,
+                op0=ALU.mult,
+                op1=ALU.min,
+                accum_out=shift[r][:, one],
+            )
             e_sb[i] = e_pool.tile([P, PROMPT], BF16, tag="e_sb", name="e_sb")
             nc.scalar.activation(
                 out=e_sb[i][:],
-                in_=ps[:],
+                in_=scaled[i][:],
                 func=ACT.Exp,
                 bias=shift[r][:, one],
-                scale=SCALE,
+                scale=-1.0,
                 accum_out=rowsum[r][:, one],
             )
 
@@ -184,11 +191,11 @@ def tile_attention_pb_kernel(tc, q_rot, pk, pv, prompt_gate, h_attn, wo, out):
             g = r % PASSES
             e_codes[r] = work.tile([P, GROUP * P], U32, tag="e_codes", name="e_codes", align_bytes=64)
             e_scales[r] = work.tile([P, GROUP * P], U8, tag="e_scales", name="e_scales", align_bytes=64)
+            weight[r] = stats.tile([P, GROUP], F32, tag="weight", name="weight")
+            nc.vector.reciprocal(out=weight[r][:], in_=rowsum[r][:])
             nc.vector.quantize_mx(
                 out=e_codes[r][:].bitcast(FP8X4), scales=e_scales[r][:], in_=e_grouped[r][:]
             )
-            weight[r] = stats.tile([P, GROUP], F32, tag="weight", name="weight")
-            nc.vector.reciprocal(out=weight[r][:], in_=rowsum[r][:])
             nc.vector.tensor_mul(
                 out=weight[r][:], in0=weight[r][:], in1=gate[:, GROUP * g : GROUP * (g + 1)]
             )
@@ -247,7 +254,7 @@ def tile_attention_pb_kernel(tc, q_rot, pk, pv, prompt_gate, h_attn, wo, out):
         def project(piece):
             rt, n = divmod(piece, D_OUT // N_TILE)
             cols = slice(N_TILE * n, N_TILE * (n + 1))
-            acc[piece] = psum_tr.tile([P, N_TILE], F32, tag="tr", name="acc")
+            acc[piece] = psum_acc.tile([P, N_TILE], F32, tag="acc", name="acc")
             for g in range(PASSES):
                 nc.tensor.matmul_mx(
                     out=acc[piece][:],
@@ -260,13 +267,11 @@ def tile_attention_pb_kernel(tc, q_rot, pk, pv, prompt_gate, h_attn, wo, out):
                 )
 
         def store(piece):
+
             rt, n = divmod(piece, D_OUT // N_TILE)
             b, t = divmod(rt, 2)
             result = results.tile([P, N_TILE], F32, tag="result")
-            if piece % 2 == 0:
-                nc.scalar.copy(out=result[:], in_=acc[piece][:])
-            else:
-                nc.vector.tensor_copy(out=result[:], in_=acc[piece][:])
+            nc.scalar.copy(out=result[:], in_=acc[piece][:])
             nc.sync.dma_start(out=out_view[b, t][:, N_TILE * n : N_TILE * (n + 1)], in_=result[:])
 
         def due(i, first, every, count):

@@ -45,10 +45,9 @@ def tile_attention_pb_kernel(tc, q_rot, pk, pv, prompt_gate, h_attn, wo, out):
         stats = ctx.enter_context(tc.tile_pool(name="stats", bufs=6))
         s_pool = ctx.enter_context(tc.tile_pool(name="s_pool", bufs=4))
         results = ctx.enter_context(tc.tile_pool(name="results", bufs=4))
-        psum_ps = ctx.enter_context(tc.psum_pool(name="psum_ps", bufs=2))
-        psum_tr = ctx.enter_context(tc.psum_pool(name="psum_tr", bufs=4))
+        psum_wide = ctx.enter_context(tc.psum_pool(name="psum_wide", bufs=4))
+        psum_tr = ctx.enter_context(tc.psum_pool(name="psum_tr", bufs=3))
         psum_num = ctx.enter_context(tc.psum_pool(name="psum_num", bufs=1))
-        psum_acc = ctx.enter_context(tc.psum_pool(name="psum_acc", bufs=1))
 
         ident_bf = keep.tile([P, P], BF16)
         make_identity(nc, ident_bf[:])
@@ -65,13 +64,6 @@ def tile_attention_pb_kernel(tc, q_rot, pk, pv, prompt_gate, h_attn, wo, out):
         fused_codes = keep.tile([P, ROW_TILES, PASSES, P], U32, align_bytes=64)
         fused_scales = keep.tile([P, ROW_TILES, PASSES, P], U8, align_bytes=64)
 
-        gate_bf = keep.tile([P, HEADS], BF16)
-        nc.sync.dma_start(
-            out=gate_bf[:], in_=prompt_gate.rearrange("a h b c -> (a h b c)").partition_broadcast(P)
-        )
-        gate = keep.tile([P, HEADS], F32)
-        nc.vector.tensor_copy(out=gate[:], in_=gate_bf[:])
-
         pk_raw, pv_raw, wo_raw, pv_grouped, wo_grouped = {}, {}, {}, {}, {}
         qT, scaled, shift, rowsum, weight = {}, {}, {}, {}, {}
         e_sb, e_grouped, e_codes, e_scales, num_ps, fused, f_grouped, acc = {}, {}, {}, {}, {}, {}, {}, {}
@@ -81,10 +73,11 @@ def tile_attention_pb_kernel(tc, q_rot, pk, pv, prompt_gate, h_attn, wo, out):
             nc.sync.dma_start(out=q_sb[:, b, heads, :], in_=q_view[b][:, heads, :])
             nc.sync.dma_start(out=ha_sb[:, b, heads, :], in_=ha_view[b][:, heads, :])
 
-        def load_prompt(g):
+        def load_group(g):
             cols = slice(K_PASS * g, K_PASS * (g + 1))
             pk_raw[g] = raw.tile([P, PROMPT // P, K_PASS], BF16, tag="pk_raw", name="pk_raw")
             nc.sync.dma_start(out=pk_raw[g][:], in_=pk_view[:, :, cols])
+            load_queries(0, g)
             pv_raw[g] = raw.tile([P, 4, K_PASS], BF16, tag="pv_raw", name="pv_raw")
             for u in range(2):
                 nc.sync.dma_start(out=pv_raw[g][:, 2 * u : 2 * u + 2, :], in_=pv_view[u][:, :, cols])
@@ -151,7 +144,7 @@ def tile_attention_pb_kernel(tc, q_rot, pk, pv, prompt_gate, h_attn, wo, out):
         def score(i):
             r, j = divmod(i, GROUP)
             one = slice(j, j + 1)
-            ps = psum_ps.tile([P, PROMPT], F32, tag="ps")
+            ps = psum_wide.tile([P, PROMPT], F32, tag="wide")
             nc.tensor.matmul(ps[:], lhsT=qT[r][:, j, :], rhs=pkT[:, i % HEADS, :], start=True, stop=True)
             scaled[i] = s_pool.tile([P, PROMPT], F32, tag="scaled", name="scaled")
             nc.vector.tensor_scalar(
@@ -254,7 +247,7 @@ def tile_attention_pb_kernel(tc, q_rot, pk, pv, prompt_gate, h_attn, wo, out):
         def project(piece):
             rt, n = divmod(piece, D_OUT // N_TILE)
             cols = slice(N_TILE * n, N_TILE * (n + 1))
-            acc[piece] = psum_acc.tile([P, N_TILE], F32, tag="acc", name="acc")
+            acc[piece] = psum_wide.tile([P, N_TILE], F32, tag="wide", name="acc")
             for g in range(PASSES):
                 nc.tensor.matmul_mx(
                     out=acc[piece][:],
@@ -271,7 +264,10 @@ def tile_attention_pb_kernel(tc, q_rot, pk, pv, prompt_gate, h_attn, wo, out):
             rt, n = divmod(piece, D_OUT // N_TILE)
             b, t = divmod(rt, 2)
             result = results.tile([P, N_TILE], F32, tag="result")
-            nc.scalar.copy(out=result[:], in_=acc[piece][:])
+            if rt == ROW_TILES - 1 and n % 2 == 1:
+                nc.vector.tensor_copy(out=result[:], in_=acc[piece][:])
+            else:
+                nc.scalar.copy(out=result[:], in_=acc[piece][:])
             nc.sync.dma_start(out=out_view[b, t][:, N_TILE * n : N_TILE * (n + 1)], in_=result[:])
 
         def due(i, first, every, count):
@@ -284,9 +280,14 @@ def tile_attention_pb_kernel(tc, q_rot, pk, pv, prompt_gate, h_attn, wo, out):
         n_tiles = D_OUT // N_TILE
 
         for g in range(2):
-            load_prompt(g)
-            load_queries(0, g)
+            load_group(g)
             load_wo(g)
+        gate_bf = keep.tile([P, HEADS], BF16)
+        nc.sync.dma_start(
+            out=gate_bf[:], in_=prompt_gate.rearrange("a h b c -> (a h b c)").partition_broadcast(P)
+        )
+        gate = keep.tile([P, HEADS], F32)
+        nc.vector.tensor_copy(out=gate[:], in_=gate_bf[:])
         flip_keys(0)
         flip_keys(1)
         flip_queries(0)
@@ -295,8 +296,7 @@ def tile_attention_pb_kernel(tc, q_rot, pk, pv, prompt_gate, h_attn, wo, out):
             ahead = due(i, -8, 4, WO_CHUNKS)
             if ahead is not None and ahead >= 2:
                 if ahead < PASSES:
-                    load_prompt(ahead)
-                    load_queries(0, ahead)
+                    load_group(ahead)
                 load_wo(ahead)
                 if PASSES <= ahead < PASSES + 2:
                     load_queries(1, 2 * (ahead - PASSES))

@@ -20,11 +20,23 @@ PASSES = K_FUSED // K_PASS
 GROUP = K_PASS // HEAD_DIM
 ROW_TILES = BATCH * SEQ // P
 N_TILE = 512
+N_TILES = D_OUT // N_TILE
 WO_CHUNK = 2 * P
 WO_CHUNKS = D_OUT // WO_CHUNK
 SCALE = 1.0 / math.sqrt(HEAD_DIM)
 
+STEPS = ROW_TILES * HEADS
+ROUNDS = STEPS // GROUP
+UNITS = WO_CHUNKS * PASSES
+LAG = 3
+PIECE_EVERY = 2
+
 FLOPS = 2 * (2 * BATCH * HEADS * SEQ * HEAD_DIM * PROMPT) + 2 * BATCH * SEQ * K_FUSED * D_OUT
+
+
+def due(step, first, every, count):
+    k, rest = divmod(step - first, every)
+    return k if rest == 0 and 0 <= k < count else None
 
 
 def tile_attention_pb_kernel(tc, q_rot, pk, pv, prompt_gate, h_attn, wo, out):
@@ -87,16 +99,18 @@ def tile_attention_pb_kernel(tc, q_rot, pk, pv, prompt_gate, h_attn, wo, out):
             nc.sync.dma_start(out=wo_raw[chunk][:], in_=wo_view[:, 2 * chunk : 2 * chunk + 2, :])
 
         def flip_keys(h):
-            g, i = divmod(h, GROUP)
+            g, j = divmod(h, GROUP)
             pkT_ps = psum_tr.tile([P, PROMPT // P, P], BF16, tag="tr")
             for c in range(PROMPT // P):
                 nc.tensor.transpose(
-                    pkT_ps[:, c, :], pk_raw[g][:, c, HEAD_DIM * i : HEAD_DIM * (i + 1)], ident_bf[:]
+                    pkT_ps[:, c, :], pk_raw[g][:, c, HEAD_DIM * j : HEAD_DIM * (j + 1)], ident_bf[:]
                 )
             nc.vector.tensor_copy(out=pkT[:, h, :], in_=pkT_ps[:].rearrange("d c p -> d (c p)"))
 
         def group_values(g):
-            pv_grouped[g] = work.tile([P, K_PASS, 4], BF16, tag="pv_grouped", name="pv_grouped", bufs=2, align_bytes=64)
+            pv_grouped[g] = work.tile(
+                [P, K_PASS, 4], BF16, tag="pv_grouped", name="pv_grouped", bufs=2, align_bytes=64
+            )
             nc.vector.tensor_copy(out=pv_grouped[g][:], in_=pv_raw[g][:].rearrange("q j c -> q c j"))
 
         def quantise_values(g):
@@ -115,7 +129,9 @@ def tile_attention_pb_kernel(tc, q_rot, pk, pv, prompt_gate, h_attn, wo, out):
                 for u in range(2):
                     first = (K_PASS * g + 2 * P * u) // 2
                     nc.tensor.transpose(woT_ps[:, n, u, :], words[:, first : first + P], ident_f32[:])
-            wo_grouped[unit] = work.tile([P, 4 * WO_CHUNK], BF16, tag="wo_grouped", name="wo_grouped", align_bytes=64)
+            wo_grouped[unit] = work.tile(
+                [P, 4 * WO_CHUNK], BF16, tag="wo_grouped", name="wo_grouped", align_bytes=64
+            )
             nc.scalar.copy(
                 out=wo_grouped[unit][:].bitcast(F32).rearrange("q (n p u) -> q n p u", n=2, u=2),
                 in_=woT_ps[:].rearrange("q n u p -> q n p u"),
@@ -169,7 +185,9 @@ def tile_attention_pb_kernel(tc, q_rot, pk, pv, prompt_gate, h_attn, wo, out):
         def flip_e(pair):
             r, half = divmod(pair, 2)
             if half == 0:
-                e_grouped[r] = work.tile([P, GROUP * P * 4], BF16, tag="e_grouped", name="e_grouped", align_bytes=64)
+                e_grouped[r] = work.tile(
+                    [P, GROUP * P * 4], BF16, tag="e_grouped", name="e_grouped", align_bytes=64
+                )
             eT_ps = psum_tr.tile([P, 2, 2, P], F32, tag="tr")
             for j in range(2):
                 words = e_sb[2 * pair + j][:].bitcast(F32)
@@ -245,7 +263,7 @@ def tile_attention_pb_kernel(tc, q_rot, pk, pv, prompt_gate, h_attn, wo, out):
             )
 
         def project(piece):
-            rt, n = divmod(piece, D_OUT // N_TILE)
+            rt, n = divmod(piece, N_TILES)
             cols = slice(N_TILE * n, N_TILE * (n + 1))
             acc[piece] = psum_wide.tile([P, N_TILE], F32, tag="wide", name="acc")
             for g in range(PASSES):
@@ -260,8 +278,7 @@ def tile_attention_pb_kernel(tc, q_rot, pk, pv, prompt_gate, h_attn, wo, out):
                 )
 
         def store(piece):
-
-            rt, n = divmod(piece, D_OUT // N_TILE)
+            rt, n = divmod(piece, N_TILES)
             b, t = divmod(rt, 2)
             result = results.tile([P, N_TILE], F32, tag="result")
             if rt == ROW_TILES - 1 and n % 2 == 1:
@@ -270,14 +287,13 @@ def tile_attention_pb_kernel(tc, q_rot, pk, pv, prompt_gate, h_attn, wo, out):
                 nc.scalar.copy(out=result[:], in_=acc[piece][:])
             nc.sync.dma_start(out=out_view[b, t][:, N_TILE * n : N_TILE * (n + 1)], in_=result[:])
 
-        def due(i, first, every, count):
-            k, rest = divmod(i - first, every)
-            return k if rest == 0 and 0 <= k < count else None
-
-        steps = ROW_TILES * HEADS
-        rounds = steps // GROUP
-        units = WO_CHUNKS * PASSES
-        n_tiles = D_OUT // N_TILE
+        e_flip = 1 + LAG
+        e_quant = GROUP - 1 + 2 * LAG
+        values = e_quant + LAG
+        f_flip = values + 1 + LAG
+        f_quant = f_flip + LAG
+        pieces_from = GROUP * (PASSES - 1) + f_quant + LAG
+        last_step = HEADS * (ROW_TILES - 1) + pieces_from + PIECE_EVERY * (N_TILES - 1)
 
         for g in range(2):
             load_group(g)
@@ -292,8 +308,8 @@ def tile_attention_pb_kernel(tc, q_rot, pk, pv, prompt_gate, h_attn, wo, out):
         flip_keys(1)
         flip_queries(0)
 
-        for i in range(steps + 28):
-            ahead = due(i, -8, 4, WO_CHUNKS)
+        for i in range(last_step + 1):
+            ahead = due(i, -2 * GROUP, GROUP, WO_CHUNKS)
             if ahead is not None and ahead >= 2:
                 if ahead < PASSES:
                     load_group(ahead)
@@ -302,49 +318,48 @@ def tile_attention_pb_kernel(tc, q_rot, pk, pv, prompt_gate, h_attn, wo, out):
                     load_queries(1, 2 * (ahead - PASSES))
                     load_queries(1, 2 * (ahead - PASSES) + 1)
 
-            r_values = due(i, 11, 4, rounds)
+            r_values = due(i, values, GROUP, ROUNDS)
             if r_values is not None:
                 multiply_values(r_values)
-            rt_piece, rest = divmod(i - 34, HEADS)
-            n_piece = due(rest, 0, 3, n_tiles)
             piece = None
-            if 0 <= rt_piece < ROW_TILES and n_piece is not None:
-                piece = n_tiles * rt_piece + n_piece
+            for rt in range(ROW_TILES):
+                n = due(i, HEADS * rt + pieces_from, PIECE_EVERY, N_TILES)
+                if n is not None:
+                    piece = N_TILES * rt + n
+            if piece is not None:
                 project(piece)
-            if i < steps:
+            if i < STEPS:
                 score(i)
-            pair = due(i, 5, 2, steps // 2)
+            pair = due(i, e_flip, 2, STEPS // 2)
             if pair is not None:
                 flip_e(pair)
-            r_fused = due(i, 16, 4, rounds)
+            r_fused = due(i, f_flip, GROUP, ROUNDS)
             if r_fused is not None:
                 flip_fused(r_fused)
-            r_next = due(i, -4, 4, rounds)
+            r_next = due(i, -GROUP, GROUP, ROUNDS)
             if r_next is not None and r_next >= 1:
                 flip_queries(r_next)
             if i + 2 < HEADS:
                 flip_keys(i + 2)
-            unit = due(i, 0, 1, units)
-            if unit is not None:
-                flip_wo(unit)
+            if i < UNITS:
+                flip_wo(i)
 
             for half in range(2):
-                r_comb = due(i, 11 + half, 4, rounds)
+                r_comb = due(i, values + half, GROUP, ROUNDS)
                 if r_comb is not None:
                     combine(r_comb, half)
-            r_e = due(i, 8, 4, rounds)
+            r_e = due(i, e_quant, GROUP, ROUNDS)
             if r_e is not None:
                 quantise_e(r_e)
-            r_q = due(i, 18, 4, rounds)
+            r_q = due(i, f_quant, GROUP, ROUNDS)
             if r_q is not None:
                 quantise_fused(r_q)
-            unit = due(i, 0 + 1, 1, units)
-            if unit is not None:
-                quantise_wo(unit)
-            g_group = due(i, 2, 4, PASSES)
+            if 1 <= i <= UNITS:
+                quantise_wo(i - 1)
+            g_group = due(i, 2, GROUP, PASSES)
             if g_group is not None:
                 group_values(g_group)
-            g_quant = due(i, 4, 4, PASSES)
+            g_quant = due(i, GROUP, GROUP, PASSES)
             if g_quant is not None:
                 quantise_values(g_quant)
             if piece is not None:

@@ -21,13 +21,14 @@ GROUP = K_PASS // HEAD_DIM
 ROW_TILES = BATCH * SEQ // P
 N_TILE = 512
 N_TILES = D_OUT // N_TILE
-WO_CHUNK = 2 * P
-WO_CHUNKS = D_OUT // WO_CHUNK
+WO_CHUNK = 4 * P
+WO_LOADS = 2 * D_OUT // WO_CHUNK
+BANK_ROWS = 2 * P
 SCALE = 1.0 / math.sqrt(HEAD_DIM)
 
 STEPS = ROW_TILES * HEADS
 ROUNDS = STEPS // GROUP
-UNITS = WO_CHUNKS * PASSES
+UNITS = D_OUT // BANK_ROWS * PASSES
 LAG = 3
 PIECE_EVERY = 2
 
@@ -37,6 +38,12 @@ FLOPS = 2 * (2 * BATCH * HEADS * SEQ * HEAD_DIM * PROMPT) + 2 * BATCH * SEQ * K_
 def due(step, first, every, count):
     k, rest = divmod(step - first, every)
     return k if rest == 0 and 0 <= k < count else None
+
+
+def fused_rounds(r):
+    if r >= ROUNDS - 2:
+        return [r]
+    return [r - 1, r] if r % 2 == 1 else []
 
 
 def tile_attention_pb_kernel(tc, q_rot, pk, pv, prompt_gate, h_attn, wo, out):
@@ -66,52 +73,79 @@ def tile_attention_pb_kernel(tc, q_rot, pk, pv, prompt_gate, h_attn, wo, out):
         ident_f32 = keep.tile([P, P], F32)
         make_identity(nc, ident_f32[:])
 
-        q_sb = keep.tile([P, BATCH, HEADS, 2 * HEAD_DIM], BF16)
         ha_sb = keep.tile([P, BATCH, HEADS, 2 * HEAD_DIM], BF16)
+        qT = keep.tile([P, BATCH, PASSES, 2, GROUP, P], BF16)
         pkT = keep.tile([P, HEADS, PROMPT], BF16)
         pv_codes = keep.tile([P, K_FUSED], U32, align_bytes=64)
         pv_scales = keep.tile([P, K_FUSED], U8, align_bytes=64)
         wo_codes = keep.tile([P, PASSES, D_OUT], U32, align_bytes=64)
         wo_scales = keep.tile([P, PASSES, D_OUT], U8, align_bytes=64)
-        fused_codes = keep.tile([P, ROW_TILES, PASSES, P], U32, align_bytes=64)
-        fused_scales = keep.tile([P, ROW_TILES, PASSES, P], U8, align_bytes=64)
+        fused_codes = keep.tile([P, ROUNDS * P], U32, align_bytes=64)
+        fused_scales = keep.tile([P, ROUNDS * P], U8, align_bytes=64)
 
-        pk_raw, pv_raw, wo_raw, pv_grouped, wo_grouped = {}, {}, {}, {}, {}
-        qT, scaled, shift, rowsum, weight = {}, {}, {}, {}, {}
+        q_raw, pk_raw, pv_raw, wo_raw, pv_grouped, wo_grouped = {}, {}, {}, {}, {}, {}
+        scaled, shift, rowsum, weight = {}, {}, {}, {}
         e_sb, e_grouped, e_codes, e_scales, num_ps, fused, f_grouped, acc = {}, {}, {}, {}, {}, {}, {}, {}
 
         def load_queries(b, g):
             heads = slice(GROUP * g, GROUP * (g + 1))
-            nc.sync.dma_start(out=q_sb[:, b, heads, :], in_=q_view[b][:, heads, :])
+            q_raw[b, g] = raw.tile([P, GROUP, 2 * HEAD_DIM], BF16, tag="q_raw", name="q_raw", bufs=4)
+            nc.sync.dma_start(out=q_raw[b, g][:], in_=q_view[b][:, heads, :])
+
+        def load_attention(b, g):
+            heads = slice(GROUP * g, GROUP * (g + 1))
             nc.sync.dma_start(out=ha_sb[:, b, heads, :], in_=ha_view[b][:, heads, :])
 
-        def load_group(g):
+        def load_keys(g, first, last):
+            if first == 0:
+                pk_raw[g] = raw.tile([P, PROMPT // P, K_PASS], BF16, tag="pk_raw", name="pk_raw")
+            cols = slice(HEAD_DIM * first, HEAD_DIM * last)
+            heads = slice(K_PASS * g + HEAD_DIM * first, K_PASS * g + HEAD_DIM * last)
+            nc.sync.dma_start(out=pk_raw[g][:, :, cols], in_=pk_view[:, :, heads])
+
+        def load_values(g):
             cols = slice(K_PASS * g, K_PASS * (g + 1))
-            pk_raw[g] = raw.tile([P, PROMPT // P, K_PASS], BF16, tag="pk_raw", name="pk_raw")
-            nc.sync.dma_start(out=pk_raw[g][:], in_=pk_view[:, :, cols])
-            load_queries(0, g)
             pv_raw[g] = raw.tile([P, 4, K_PASS], BF16, tag="pv_raw", name="pv_raw")
             for u in range(2):
                 nc.sync.dma_start(out=pv_raw[g][:, 2 * u : 2 * u + 2, :], in_=pv_view[u][:, :, cols])
 
-        def load_wo(chunk):
-            wo_raw[chunk] = raw.tile([P, WO_CHUNK // P, K_FUSED], BF16, tag="wo_raw", name="wo_raw")
-            nc.sync.dma_start(out=wo_raw[chunk][:], in_=wo_view[:, 2 * chunk : 2 * chunk + 2, :])
-
-        def flip_keys(h):
-            g, j = divmod(h, GROUP)
-            pkT_ps = psum_tr.tile([P, PROMPT // P, P], BF16, tag="tr")
-            for c in range(PROMPT // P):
-                nc.tensor.transpose(
-                    pkT_ps[:, c, :], pk_raw[g][:, c, HEAD_DIM * j : HEAD_DIM * (j + 1)], ident_bf[:]
+        def load_wo(load):
+            chunk, k_half = divmod(load, 2)
+            blocks = WO_CHUNK // P
+            wo_raw[load] = raw.tile([P, blocks, K_FUSED // 2], BF16, tag="wo_raw", name="wo_raw")
+            k_cols = slice(K_FUSED // 2 * k_half, K_FUSED // 2 * (k_half + 1))
+            for n in range(0, blocks, 2):
+                nc.sync.dma_start(
+                    out=wo_raw[load][:, n : n + 2, :],
+                    in_=wo_view[:, blocks * chunk + n : blocks * chunk + n + 2, k_cols],
                 )
-            nc.vector.tensor_copy(out=pkT[:, h, :], in_=pkT_ps[:].rearrange("d c p -> d (c p)"))
+
+        def flip_keys(h, heads):
+            g, j = divmod(h, GROUP)
+            pkT_ps = psum_tr.tile([P, heads, PROMPT // P, P], BF16, tag="tr", name="pkT_ps")
+            for n in range(heads):
+                for c in range(PROMPT // P):
+                    nc.tensor.transpose(
+                        pkT_ps[:, n, c, :],
+                        pk_raw[g][:, c, HEAD_DIM * (j + n) : HEAD_DIM * (j + n + 1)],
+                        ident_bf[:],
+                    )
+            nc.vector.tensor_copy(out=pkT[:, h : h + heads, :], in_=pkT_ps[:].rearrange("d n c p -> d n (c p)"))
 
         def group_values(g):
             pv_grouped[g] = work.tile(
-                [P, K_PASS, 4], BF16, tag="pv_grouped", name="pv_grouped", bufs=2, align_bytes=64
+                [P, K_PASS, 4], BF16, tag="pv_grouped", name="pv_grouped", bufs=1, align_bytes=64
             )
-            nc.vector.tensor_copy(out=pv_grouped[g][:], in_=pv_raw[g][:].rearrange("q j c -> q c j"))
+            for h in range(GROUP):
+                cols = slice(HEAD_DIM * h, HEAD_DIM * (h + 1))
+                nc.gpsimd.tensor_scalar(
+                    out=pv_grouped[g][:, cols, :],
+                    in0=pv_raw[g][:, :, cols].rearrange("q j c -> q c j"),
+                    scalar1=1.0,
+                    scalar2=0.0,
+                    op0=ALU.mult,
+                    op1=ALU.add,
+                )
 
         def quantise_values(g):
             cols = slice(K_PASS * g, K_PASS * (g + 1))
@@ -122,46 +156,58 @@ def tile_attention_pb_kernel(tc, q_rot, pk, pv, prompt_gate, h_attn, wo, out):
             )
 
         def flip_wo(unit):
-            chunk, g = divmod(unit, PASSES)
+            tile, half = divmod(unit, 2)
             woT_ps = psum_tr.tile([P, 2, 2, P], F32, tag="tr")
             for n in range(2):
-                words = wo_raw[chunk][:, n, :].bitcast(F32)
+                words = wo_raw[tile // 2][:, 2 * half + n, :].bitcast(F32)
                 for u in range(2):
-                    first = (K_PASS * g + 2 * P * u) // 2
+                    first = (K_PASS * (tile % 2) + 2 * P * u) // 2
                     nc.tensor.transpose(woT_ps[:, n, u, :], words[:, first : first + P], ident_f32[:])
-            wo_grouped[unit] = work.tile(
-                [P, 4 * WO_CHUNK], BF16, tag="wo_grouped", name="wo_grouped", align_bytes=64
-            )
-            nc.scalar.copy(
-                out=wo_grouped[unit][:].bitcast(F32).rearrange("q (n p u) -> q n p u", n=2, u=2),
+            if half == 0:
+                wo_grouped[tile] = work.tile(
+                    [P, 4 * WO_CHUNK], BF16, tag="wo_grouped", name="wo_grouped", align_bytes=64
+                )
+            grouped = wo_grouped[tile][:].bitcast(F32)[:, 2 * BANK_ROWS * half : 2 * BANK_ROWS * (half + 1)]
+            copy = nc.vector.tensor_copy if unit % 4 == 3 else nc.scalar.copy
+            copy(
+                out=grouped.rearrange("q (n p u) -> q n p u", n=2, u=2),
                 in_=woT_ps[:].rearrange("q n u p -> q n p u"),
             )
 
-        def quantise_wo(unit):
-            chunk, g = divmod(unit, PASSES)
+        def quantise_wo(tile):
+            chunk, g = divmod(tile, PASSES)
             cols = slice(WO_CHUNK * chunk, WO_CHUNK * (chunk + 1))
             nc.vector.quantize_mx(
-                out=wo_codes[:, g, cols].bitcast(FP8X4), scales=wo_scales[:, g, cols], in_=wo_grouped[unit][:]
+                out=wo_codes[:, g, cols].bitcast(FP8X4),
+                scales=wo_scales[:, g, cols],
+                in_=wo_grouped[tile][:],
             )
 
-        def flip_queries(r):
-            rt, g = divmod(r, PASSES)
-            b, t = divmod(rt, 2)
-            qT_ps = psum_tr.tile([P, GROUP, P], BF16, tag="tr")
-            for j in range(GROUP):
-                nc.tensor.transpose(
-                    qT_ps[:, j, :], q_sb[:, b, GROUP * g + j, HEAD_DIM * t : HEAD_DIM * (t + 1)], ident_bf[:]
-                )
-            qT[r] = stats.tile([P, GROUP, P], BF16, tag="qT", name="qT")
-            nc.vector.tensor_copy(out=qT[r][:], in_=qT_ps[:])
+        def flip_queries(r, tiles, copy):
+            b, g = divmod(r, PASSES)
+            qT_ps = psum_tr.tile([P, len(tiles), GROUP, P], BF16, tag="tr", name="qT_ps")
+            for t in tiles:
+                for j in range(GROUP):
+                    nc.tensor.transpose(
+                        qT_ps[:, t - tiles[0], j, :],
+                        q_raw[b, g][:, j, HEAD_DIM * t : HEAD_DIM * (t + 1)],
+                        ident_bf[:],
+                    )
+            copy(out=qT[:, b, g, tiles[0] : tiles[0] + len(tiles), :, :], in_=qT_ps[:])
+
+        def open_round(r):
             shift[r] = stats.tile([P, GROUP], F32, tag="shift", name="shift")
             rowsum[r] = stats.tile([P, GROUP], F32, tag="rowsum", name="rowsum")
 
         def score(i):
             r, j = divmod(i, GROUP)
+            rt, g = divmod(r, PASSES)
+            b, t = divmod(rt, 2)
             one = slice(j, j + 1)
+            if j == 0:
+                open_round(r)
             ps = psum_wide.tile([P, PROMPT], F32, tag="wide")
-            nc.tensor.matmul(ps[:], lhsT=qT[r][:, j, :], rhs=pkT[:, i % HEADS, :], start=True, stop=True)
+            nc.tensor.matmul(ps[:], lhsT=qT[:, b, g, t, j, :], rhs=pkT[:, i % HEADS, :], start=True, stop=True)
             scaled[i] = s_pool.tile([P, PROMPT], F32, tag="scaled", name="scaled")
             nc.vector.tensor_scalar(
                 out=scaled[i][:],
@@ -203,13 +249,14 @@ def tile_attention_pb_kernel(tc, q_rot, pk, pv, prompt_gate, h_attn, wo, out):
             e_codes[r] = work.tile([P, GROUP * P], U32, tag="e_codes", name="e_codes", align_bytes=64)
             e_scales[r] = work.tile([P, GROUP * P], U8, tag="e_scales", name="e_scales", align_bytes=64)
             weight[r] = stats.tile([P, GROUP], F32, tag="weight", name="weight")
-            nc.vector.reciprocal(out=weight[r][:], in_=rowsum[r][:])
+            divisor = stats.tile([P, GROUP], F32, tag="divisor")
+            nc.gpsimd.tensor_mul(
+                out=divisor[:], in0=rowsum[r][:], in1=inverse_gate[:, GROUP * g : GROUP * (g + 1)]
+            )
             nc.vector.quantize_mx(
                 out=e_codes[r][:].bitcast(FP8X4), scales=e_scales[r][:], in_=e_grouped[r][:]
             )
-            nc.vector.tensor_mul(
-                out=weight[r][:], in0=weight[r][:], in1=gate[:, GROUP * g : GROUP * (g + 1)]
-            )
+            nc.vector.reciprocal(out=weight[r][:], in_=divisor[:])
 
         def multiply_values(r):
             g = r % PASSES
@@ -243,23 +290,27 @@ def tile_attention_pb_kernel(tc, q_rot, pk, pv, prompt_gate, h_attn, wo, out):
                 )
 
         def flip_fused(r):
-            fT_ps = psum_tr.tile([P, 2, P], F32, tag="tr")
-            for u in range(2):
-                nc.tensor.transpose(
-                    fT_ps[:, u, :], fused[r][:].bitcast(F32)[:, P * u : P * (u + 1)], ident_f32[:]
-                )
-            f_grouped[r] = work.tile([P, P * 4], BF16, tag="f_grouped", name="f_grouped", align_bytes=64)
+            rounds = fused_rounds(r)
+            n_rounds = len(rounds)
+            fT_ps = psum_tr.tile([P, n_rounds, 2, P], F32, tag="tr", name="fT_ps")
+            for n, one in enumerate(rounds):
+                for u in range(2):
+                    nc.tensor.transpose(
+                        fT_ps[:, n, u, :], fused[one][:].bitcast(F32)[:, P * u : P * (u + 1)], ident_f32[:]
+                    )
+            f_grouped[r] = work.tile(
+                [P, n_rounds * P * 4], BF16, tag="f_grouped", name="f_grouped", align_bytes=64
+            )
             nc.scalar.copy(
-                out=f_grouped[r][:].bitcast(F32).rearrange("q (m u) -> q m u", u=2),
-                in_=fT_ps[:].rearrange("q u m -> q m u"),
+                out=f_grouped[r][:].bitcast(F32).rearrange("q (n m u) -> q n m u", n=n_rounds, u=2),
+                in_=fT_ps[:].rearrange("q n u m -> q n m u"),
             )
 
         def quantise_fused(r):
-            rt, g = divmod(r, PASSES)
+            rounds = fused_rounds(r)
+            cols = slice(P * rounds[0], P * (r + 1))
             nc.vector.quantize_mx(
-                out=fused_codes[:, rt, g, :].bitcast(FP8X4),
-                scales=fused_scales[:, rt, g, :],
-                in_=f_grouped[r][:],
+                out=fused_codes[:, cols].bitcast(FP8X4), scales=fused_scales[:, cols], in_=f_grouped[r][:]
             )
 
         def project(piece):
@@ -267,10 +318,11 @@ def tile_attention_pb_kernel(tc, q_rot, pk, pv, prompt_gate, h_attn, wo, out):
             cols = slice(N_TILE * n, N_TILE * (n + 1))
             acc[piece] = psum_wide.tile([P, N_TILE], F32, tag="wide", name="acc")
             for g in range(PASSES):
+                f_cols = slice(P * (PASSES * rt + g), P * (PASSES * rt + g + 1))
                 nc.tensor.matmul_mx(
                     out=acc[piece][:],
-                    lhsT=fused_codes[:, rt, g, :].bitcast(FP8X4),
-                    lhsT_scale=fused_scales[:, rt, g, :],
+                    lhsT=fused_codes[:, f_cols].bitcast(FP8X4),
+                    lhsT_scale=fused_scales[:, f_cols],
                     rhs=wo_codes[:, g, cols].bitcast(FP8X4),
                     rhs_scale=wo_scales[:, g, cols],
                     start=(g == 0),
@@ -295,28 +347,39 @@ def tile_attention_pb_kernel(tc, q_rot, pk, pv, prompt_gate, h_attn, wo, out):
         pieces_from = GROUP * (PASSES - 1) + f_quant + LAG
         last_step = HEADS * (ROW_TILES - 1) + pieces_from + PIECE_EVERY * (N_TILES - 1)
 
-        for g in range(2):
-            load_group(g)
-            load_wo(g)
+        load_keys(0, 0, 2)
+        load_queries(0, 0)
+        load_wo(0)
+        load_keys(0, 2, GROUP)
+        load_values(0)
+        load_keys(1, 0, GROUP)
+        load_queries(0, 1)
+        load_wo(1)
+        load_attention(0, 0)
+        load_values(1)
+        load_attention(0, 1)
         gate_bf = keep.tile([P, HEADS], BF16)
         nc.sync.dma_start(
             out=gate_bf[:], in_=prompt_gate.rearrange("a h b c -> (a h b c)").partition_broadcast(P)
         )
-        gate = keep.tile([P, HEADS], F32)
-        nc.vector.tensor_copy(out=gate[:], in_=gate_bf[:])
-        flip_keys(0)
-        flip_keys(1)
-        flip_queries(0)
+        inverse_gate = keep.tile([P, HEADS], F32)
+        flip_keys(0, 1)
+        flip_queries(0, [0], nc.scalar.copy)
+        flip_keys(1, 1)
 
         for i in range(last_step + 1):
-            ahead = due(i, -2 * GROUP, GROUP, WO_CHUNKS)
+            ahead = due(i, -2 * GROUP, GROUP, WO_LOADS)
             if ahead is not None and ahead >= 2:
                 if ahead < PASSES:
-                    load_group(ahead)
+                    load_keys(ahead, 0, GROUP)
+                    load_queries(0, ahead)
+                    load_values(ahead)
+                    load_attention(0, ahead)
                 load_wo(ahead)
                 if PASSES <= ahead < PASSES + 2:
-                    load_queries(1, 2 * (ahead - PASSES))
-                    load_queries(1, 2 * (ahead - PASSES) + 1)
+                    for g in (2 * (ahead - PASSES), 2 * (ahead - PASSES) + 1):
+                        load_queries(1, g)
+                        load_attention(1, g)
 
             r_values = due(i, values, GROUP, ROUNDS)
             if r_values is not None:
@@ -334,13 +397,16 @@ def tile_attention_pb_kernel(tc, q_rot, pk, pv, prompt_gate, h_attn, wo, out):
             if pair is not None:
                 flip_e(pair)
             r_fused = due(i, f_flip, GROUP, ROUNDS)
-            if r_fused is not None:
+            if r_fused is not None and fused_rounds(r_fused):
                 flip_fused(r_fused)
-            r_next = due(i, -GROUP, GROUP, ROUNDS)
-            if r_next is not None and r_next >= 1:
-                flip_queries(r_next)
-            if i + 2 < HEADS:
-                flip_keys(i + 2)
+            for b in range(BATCH):
+                g_next = due(i, 2 * HEADS * b - GROUP, GROUP, PASSES)
+                if g_next is not None and (b > 0 or g_next >= 1):
+                    flip_queries(PASSES * b + g_next, [0, 1], nc.vector.tensor_copy)
+            if i == 2:
+                flip_queries(0, [1], nc.vector.tensor_copy)
+            if i % 2 == 0 and i + 2 < HEADS:
+                flip_keys(i + 2, 2)
             if i < UNITS:
                 flip_wo(i)
 
@@ -350,12 +416,15 @@ def tile_attention_pb_kernel(tc, q_rot, pk, pv, prompt_gate, h_attn, wo, out):
                     combine(r_comb, half)
             r_e = due(i, e_quant, GROUP, ROUNDS)
             if r_e is not None:
+                if r_e == 0:
+                    nc.vector.reciprocal(out=inverse_gate[:], in_=gate_bf[:])
                 quantise_e(r_e)
             r_q = due(i, f_quant, GROUP, ROUNDS)
-            if r_q is not None:
+            if r_q is not None and fused_rounds(r_q):
                 quantise_fused(r_q)
-            if 1 <= i <= UNITS:
-                quantise_wo(i - 1)
+            tile = due(i, 2, 2, UNITS // 2)
+            if tile is not None:
+                quantise_wo(tile)
             g_group = due(i, 2, GROUP, PASSES)
             if g_group is not None:
                 group_values(g_group)

@@ -21,16 +21,54 @@ GROUP = K_PASS // HEAD_DIM
 ROW_TILES = BATCH * SEQ // P
 N_TILE = 512
 N_TILES = D_OUT // N_TILE
-WO_CHUNK = 4 * P
-WO_LOADS = 2 * D_OUT // WO_CHUNK
 BANK_ROWS = 2 * P
 SCALE = 1.0 / math.sqrt(HEAD_DIM)
 
+LAGS = (6, 10, 11, 13, 14, 16)
+SINGLES = 4
+PEV = 2
+QPH = 3
+PVQ = 5
+PVG = 3
+MAXFIRST = False
+MAXLAST = False
+EXPFIRST = False
+Q_ON_SCALAR = False
+
+
+def WO_STEP(u):
+    return 2 * u + 3 if u < 8 else 18 + u - 8 if u < 20 else 30 + (4 * (u - 20) + 2) // 3
+
+
+def WO_LOAD(l):
+    return max(1, WO_STEP(4 * l) - 9)
+
+
+def PV_ON_SCALAR(g):
+    return False
+
+
+def KEYS_ON_SCALAR(i):
+    return True
+
+
+def WO_ON_VECTOR(unit):
+    return False
+
+
+def OUT_ON_VECTOR(piece):
+    return False
+
+
+EL = 2
+EPB = 9
+WQ = 3
+WOB = 6
+WRB = 3
+LPG = (-3, -2, 0, 1)
 STEPS = ROW_TILES * HEADS
 ROUNDS = STEPS // GROUP
 UNITS = D_OUT // BANK_ROWS * PASSES
-LAG = 3
-PIECE_EVERY = 2
 
 FLOPS = 2 * (2 * BATCH * HEADS * SEQ * HEAD_DIM * PROMPT) + 2 * BATCH * SEQ * K_FUSED * D_OUT
 
@@ -41,9 +79,13 @@ def due(step, first, every, count):
 
 
 def fused_rounds(r):
-    if r >= ROUNDS - 2:
+    if r >= ROUNDS - SINGLES:
         return [r]
     return [r - 1, r] if r % 2 == 1 else []
+
+
+def wo_unit_step(unit):
+    return WO_STEP(unit)
 
 
 def tile_attention_pb_kernel(tc, q_rot, pk, pv, prompt_gate, h_attn, wo, out):
@@ -60,12 +102,11 @@ def tile_attention_pb_kernel(tc, q_rot, pk, pv, prompt_gate, h_attn, wo, out):
         keep = ctx.enter_context(tc.tile_pool(name="keep", bufs=1))
         raw = ctx.enter_context(tc.tile_pool(name="raw", bufs=3))
         work = ctx.enter_context(tc.tile_pool(name="work", bufs=3))
-        e_pool = ctx.enter_context(tc.tile_pool(name="e_pool", bufs=8))
+        e_pool = ctx.enter_context(tc.tile_pool(name="e_pool", bufs=EPB))
         stats = ctx.enter_context(tc.tile_pool(name="stats", bufs=6))
         s_pool = ctx.enter_context(tc.tile_pool(name="s_pool", bufs=4))
         results = ctx.enter_context(tc.tile_pool(name="results", bufs=4))
-        psum_wide = ctx.enter_context(tc.psum_pool(name="psum_wide", bufs=4))
-        psum_tr = ctx.enter_context(tc.psum_pool(name="psum_tr", bufs=3))
+        psum_any = ctx.enter_context(tc.psum_pool(name="psum_any", bufs=7))
         psum_num = ctx.enter_context(tc.psum_pool(name="psum_num", bufs=1))
 
         ident_bf = keep.tile([P, P], BF16)
@@ -74,7 +115,6 @@ def tile_attention_pb_kernel(tc, q_rot, pk, pv, prompt_gate, h_attn, wo, out):
         make_identity(nc, ident_f32[:])
 
         ha_sb = keep.tile([P, BATCH, HEADS, 2 * HEAD_DIM], BF16)
-        qT = keep.tile([P, BATCH, PASSES, 2, GROUP, P], BF16)
         pkT = keep.tile([P, HEADS, PROMPT], BF16)
         pv_codes = keep.tile([P, K_FUSED], U32, align_bytes=64)
         pv_scales = keep.tile([P, K_FUSED], U8, align_bytes=64)
@@ -82,9 +122,11 @@ def tile_attention_pb_kernel(tc, q_rot, pk, pv, prompt_gate, h_attn, wo, out):
         wo_scales = keep.tile([P, PASSES, D_OUT], U8, align_bytes=64)
         fused_codes = keep.tile([P, ROUNDS * P], U32, align_bytes=64)
         fused_scales = keep.tile([P, ROUNDS * P], U8, align_bytes=64)
+        gate_bf = keep.tile([P, HEADS], BF16)
+        inverse_gate = keep.tile([P, HEADS], F32)
 
         q_raw, pk_raw, pv_raw, wo_raw, pv_grouped, wo_grouped = {}, {}, {}, {}, {}, {}
-        scaled, shift, rowsum, weight = {}, {}, {}, {}
+        banks, qT, scaled, shift, rowsum, weight = {}, {}, {}, {}, {}, {}
         e_sb, e_grouped, e_codes, e_scales, num_ps, fused, f_grouped, acc = {}, {}, {}, {}, {}, {}, {}, {}
 
         def load_queries(b, g):
@@ -110,153 +152,69 @@ def tile_attention_pb_kernel(tc, q_rot, pk, pv, prompt_gate, h_attn, wo, out):
                 nc.sync.dma_start(out=pv_raw[g][:, 2 * u : 2 * u + 2, :], in_=pv_view[u][:, :, cols])
 
         def load_wo(load):
-            chunk, k_half = divmod(load, 2)
-            blocks = WO_CHUNK // P
-            wo_raw[load] = raw.tile([P, blocks, K_FUSED // 2], BF16, tag="wo_raw", name="wo_raw")
-            k_cols = slice(K_FUSED // 2 * k_half, K_FUSED // 2 * (k_half + 1))
-            for n in range(0, blocks, 2):
-                nc.sync.dma_start(
-                    out=wo_raw[load][:, n : n + 2, :],
-                    in_=wo_view[:, blocks * chunk + n : blocks * chunk + n + 2, k_cols],
-                )
+            wo_raw[load] = raw.tile([P, 2, K_FUSED], BF16, tag="wo_raw", name="wo_raw", bufs=WRB)
+            nc.sync.dma_start(out=wo_raw[load][:], in_=wo_view[:, 2 * load : 2 * load + 2, :])
 
         def flip_keys(h, heads):
             g, j = divmod(h, GROUP)
-            pkT_ps = psum_tr.tile([P, heads, PROMPT // P, P], BF16, tag="tr", name="pkT_ps")
+            banks["keys", h] = psum_any.tile([P, heads, PROMPT // P, P], BF16, tag="bank", name="pkT_ps")
             for n in range(heads):
                 for c in range(PROMPT // P):
                     nc.tensor.transpose(
-                        pkT_ps[:, n, c, :],
+                        banks["keys", h][:, n, c, :],
                         pk_raw[g][:, c, HEAD_DIM * (j + n) : HEAD_DIM * (j + n + 1)],
                         ident_bf[:],
                     )
-            nc.vector.tensor_copy(out=pkT[:, h : h + heads, :], in_=pkT_ps[:].rearrange("d n c p -> d n (c p)"))
 
-        def group_values(g):
-            pv_grouped[g] = work.tile(
-                [P, K_PASS, 4], BF16, tag="pv_grouped", name="pv_grouped", bufs=1, align_bytes=64
+        def flip_queries(b, g, tiles):
+            banks["queries", b, g, tiles[0]] = psum_any.tile(
+                [P, len(tiles), GROUP, P], BF16, tag="bank", name="qT_ps"
             )
-            for h in range(GROUP):
-                cols = slice(HEAD_DIM * h, HEAD_DIM * (h + 1))
-                nc.gpsimd.tensor_scalar(
-                    out=pv_grouped[g][:, cols, :],
-                    in0=pv_raw[g][:, :, cols].rearrange("q j c -> q c j"),
-                    scalar1=1.0,
-                    scalar2=0.0,
-                    op0=ALU.mult,
-                    op1=ALU.add,
-                )
-
-        def quantise_values(g):
-            cols = slice(K_PASS * g, K_PASS * (g + 1))
-            nc.vector.quantize_mx(
-                out=pv_codes[:, cols].bitcast(FP8X4),
-                scales=pv_scales[:, cols],
-                in_=pv_grouped[g][:].rearrange("q c j -> q (c j)"),
-            )
-
-        def flip_wo(unit):
-            tile, half = divmod(unit, 2)
-            woT_ps = psum_tr.tile([P, 2, 2, P], F32, tag="tr")
-            for n in range(2):
-                words = wo_raw[tile // 2][:, 2 * half + n, :].bitcast(F32)
-                for u in range(2):
-                    first = (K_PASS * (tile % 2) + 2 * P * u) // 2
-                    nc.tensor.transpose(woT_ps[:, n, u, :], words[:, first : first + P], ident_f32[:])
-            if half == 0:
-                wo_grouped[tile] = work.tile(
-                    [P, 4 * WO_CHUNK], BF16, tag="wo_grouped", name="wo_grouped", align_bytes=64
-                )
-            grouped = wo_grouped[tile][:].bitcast(F32)[:, 2 * BANK_ROWS * half : 2 * BANK_ROWS * (half + 1)]
-            copy = nc.vector.tensor_copy if unit % 4 == 3 else nc.scalar.copy
-            copy(
-                out=grouped.rearrange("q (n p u) -> q n p u", n=2, u=2),
-                in_=woT_ps[:].rearrange("q n u p -> q n p u"),
-            )
-
-        def quantise_wo(tile):
-            chunk, g = divmod(tile, PASSES)
-            cols = slice(WO_CHUNK * chunk, WO_CHUNK * (chunk + 1))
-            nc.vector.quantize_mx(
-                out=wo_codes[:, g, cols].bitcast(FP8X4),
-                scales=wo_scales[:, g, cols],
-                in_=wo_grouped[tile][:],
-            )
-
-        def flip_queries(r, tiles, copy):
-            b, g = divmod(r, PASSES)
-            qT_ps = psum_tr.tile([P, len(tiles), GROUP, P], BF16, tag="tr", name="qT_ps")
             for t in tiles:
                 for j in range(GROUP):
                     nc.tensor.transpose(
-                        qT_ps[:, t - tiles[0], j, :],
+                        banks["queries", b, g, tiles[0]][:, t - tiles[0], j, :],
                         q_raw[b, g][:, j, HEAD_DIM * t : HEAD_DIM * (t + 1)],
                         ident_bf[:],
                     )
-            copy(out=qT[:, b, g, tiles[0] : tiles[0] + len(tiles), :, :], in_=qT_ps[:])
 
-        def open_round(r):
-            shift[r] = stats.tile([P, GROUP], F32, tag="shift", name="shift")
-            rowsum[r] = stats.tile([P, GROUP], F32, tag="rowsum", name="rowsum")
+        def flip_wo(unit):
+            chunk, g = divmod(unit, PASSES)
+            banks["wo", unit] = psum_any.tile([P, 2, 2, P], F32, tag="bank", name="woT_ps")
+            for n in range(2):
+                words = wo_raw[chunk][:, n, :].bitcast(F32)
+                for u in range(2):
+                    first = (K_PASS * g + 2 * P * u) // 2
+                    nc.tensor.transpose(
+                        banks["wo", unit][:, n, u, :], words[:, first : first + P], ident_f32[:]
+                    )
 
         def score(i):
             r, j = divmod(i, GROUP)
             rt, g = divmod(r, PASSES)
             b, t = divmod(rt, 2)
-            one = slice(j, j + 1)
-            if j == 0:
-                open_round(r)
-            ps = psum_wide.tile([P, PROMPT], F32, tag="wide")
-            nc.tensor.matmul(ps[:], lhsT=qT[:, b, g, t, j, :], rhs=pkT[:, i % HEADS, :], start=True, stop=True)
-            scaled[i] = s_pool.tile([P, PROMPT], F32, tag="scaled", name="scaled")
-            nc.vector.tensor_scalar(
-                out=scaled[i][:],
-                in0=ps[:],
-                scalar1=-SCALE,
-                scalar2=None,
-                op0=ALU.mult,
-                op1=ALU.min,
-                accum_out=shift[r][:, one],
-            )
-            e_sb[i] = e_pool.tile([P, PROMPT], BF16, tag="e_sb", name="e_sb")
-            nc.scalar.activation(
-                out=e_sb[i][:],
-                in_=scaled[i][:],
-                func=ACT.Exp,
-                bias=shift[r][:, one],
-                scale=-1.0,
-                accum_out=rowsum[r][:, one],
+            banks["score", i] = psum_any.tile([P, PROMPT], F32, tag="bank", name="score_ps")
+            nc.tensor.matmul(
+                banks["score", i][:], lhsT=qT[b, g][:, t, j, :], rhs=pkT[:, i % HEADS, :], start=True, stop=True
             )
 
         def flip_e(pair):
-            r, half = divmod(pair, 2)
-            if half == 0:
-                e_grouped[r] = work.tile(
-                    [P, GROUP * P * 4], BF16, tag="e_grouped", name="e_grouped", align_bytes=64
-                )
-            eT_ps = psum_tr.tile([P, 2, 2, P], F32, tag="tr")
+            banks["e", pair] = psum_any.tile([P, 2, 2, P], F32, tag="bank", name="eT_ps")
             for j in range(2):
                 words = e_sb[2 * pair + j][:].bitcast(F32)
                 for u in range(2):
-                    nc.tensor.transpose(eT_ps[:, j, u, :], words[:, P * u : P * (u + 1)], ident_f32[:])
-            e_words = e_grouped[r][:].bitcast(F32).rearrange("q (j m u) -> q j m u", j=GROUP, u=2)
-            nc.scalar.copy(
-                out=e_words[:, 2 * half : 2 * half + 2, :, :], in_=eT_ps[:].rearrange("q j u m -> q j m u")
-            )
+                    nc.tensor.transpose(banks["e", pair][:, j, u, :], words[:, P * u : P * (u + 1)], ident_f32[:])
 
-        def quantise_e(r):
-            g = r % PASSES
-            e_codes[r] = work.tile([P, GROUP * P], U32, tag="e_codes", name="e_codes", align_bytes=64)
-            e_scales[r] = work.tile([P, GROUP * P], U8, tag="e_scales", name="e_scales", align_bytes=64)
-            weight[r] = stats.tile([P, GROUP], F32, tag="weight", name="weight")
-            divisor = stats.tile([P, GROUP], F32, tag="divisor")
-            nc.gpsimd.tensor_mul(
-                out=divisor[:], in0=rowsum[r][:], in1=inverse_gate[:, GROUP * g : GROUP * (g + 1)]
-            )
-            nc.vector.quantize_mx(
-                out=e_codes[r][:].bitcast(FP8X4), scales=e_scales[r][:], in_=e_grouped[r][:]
-            )
-            nc.vector.reciprocal(out=weight[r][:], in_=divisor[:])
+        def flip_fused(r):
+            rounds = fused_rounds(r)
+            banks["fused", r] = psum_any.tile([P, len(rounds), 2, P], F32, tag="bank", name="fT_ps")
+            for n, one in enumerate(rounds):
+                for u in range(2):
+                    nc.tensor.transpose(
+                        banks["fused", r][:, n, u, :],
+                        fused[one][:].bitcast(F32)[:, P * u : P * (u + 1)],
+                        ident_f32[:],
+                    )
 
         def multiply_values(r):
             g = r % PASSES
@@ -274,50 +232,12 @@ def tile_attention_pb_kernel(tc, q_rot, pk, pv, prompt_gate, h_attn, wo, out):
                     stop=True,
                 )
 
-        def combine(r, half):
-            rt, g = divmod(r, PASSES)
-            b, t = divmod(rt, 2)
-            if half == 0:
-                fused[r] = work.tile([P, K_PASS], BF16, tag="fused", name="fused")
-            for j in range(2 * half, 2 * half + 2):
-                nc.vector.scalar_tensor_tensor(
-                    out=fused[r][:, HEAD_DIM * j : HEAD_DIM * (j + 1)],
-                    in0=num_ps[r][:, j, :],
-                    scalar=weight[r][:, j : j + 1],
-                    in1=ha_sb[:, b, GROUP * g + j, HEAD_DIM * t : HEAD_DIM * (t + 1)],
-                    op0=ALU.mult,
-                    op1=ALU.add,
-                )
-
-        def flip_fused(r):
-            rounds = fused_rounds(r)
-            n_rounds = len(rounds)
-            fT_ps = psum_tr.tile([P, n_rounds, 2, P], F32, tag="tr", name="fT_ps")
-            for n, one in enumerate(rounds):
-                for u in range(2):
-                    nc.tensor.transpose(
-                        fT_ps[:, n, u, :], fused[one][:].bitcast(F32)[:, P * u : P * (u + 1)], ident_f32[:]
-                    )
-            f_grouped[r] = work.tile(
-                [P, n_rounds * P * 4], BF16, tag="f_grouped", name="f_grouped", align_bytes=64
-            )
-            nc.scalar.copy(
-                out=f_grouped[r][:].bitcast(F32).rearrange("q (n m u) -> q n m u", n=n_rounds, u=2),
-                in_=fT_ps[:].rearrange("q n u m -> q n m u"),
-            )
-
-        def quantise_fused(r):
-            rounds = fused_rounds(r)
-            cols = slice(P * rounds[0], P * (r + 1))
-            nc.vector.quantize_mx(
-                out=fused_codes[:, cols].bitcast(FP8X4), scales=fused_scales[:, cols], in_=f_grouped[r][:]
-            )
-
-        def project(piece):
+        def project(piece, passes):
             rt, n = divmod(piece, N_TILES)
             cols = slice(N_TILE * n, N_TILE * (n + 1))
-            acc[piece] = psum_wide.tile([P, N_TILE], F32, tag="wide", name="acc")
-            for g in range(PASSES):
+            if passes[0] == 0:
+                acc[piece] = psum_any.tile([P, N_TILE], F32, tag="bank", name="acc")
+            for g in passes:
                 f_cols = slice(P * (PASSES * rt + g), P * (PASSES * rt + g + 1))
                 nc.tensor.matmul_mx(
                     out=acc[piece][:],
@@ -329,107 +249,312 @@ def tile_attention_pb_kernel(tc, q_rot, pk, pv, prompt_gate, h_attn, wo, out):
                     stop=(g == PASSES - 1),
                 )
 
-        def store(piece):
+        def empty_keys(h, heads, copy):
+            copy(out=pkT[:, h : h + heads, :], in_=banks["keys", h][:].rearrange("d n c p -> d n (c p)"))
+
+        def empty_queries(b, g, tiles, copy):
+            if tiles[0] == 0:
+                qT[b, g] = raw.tile([P, 2, GROUP, P], BF16, tag="qT", name="qT", bufs=6)
+            copy(out=qT[b, g][:, tiles[0] : tiles[0] + len(tiles), :, :], in_=banks["queries", b, g, tiles[0]][:])
+
+        def empty_wo(unit, copy):
+            wo_grouped[unit] = work.tile(
+                [P, 4 * BANK_ROWS], BF16, tag="wo_grouped", name="wo_grouped", bufs=WOB, align_bytes=64
+            )
+            copy(
+                out=wo_grouped[unit][:].bitcast(F32).rearrange("q (n p u) -> q n p u", n=2, u=2),
+                in_=banks["wo", unit][:].rearrange("q n u p -> q n p u"),
+            )
+
+        def quantise_wo(unit):
+            chunk, g = divmod(unit, PASSES)
+            cols = slice(BANK_ROWS * chunk, BANK_ROWS * (chunk + 1))
+            nc.vector.quantize_mx(
+                out=wo_codes[:, g, cols].bitcast(FP8X4),
+                scales=wo_scales[:, g, cols],
+                in_=wo_grouped[unit][:],
+            )
+
+        def group_values(g, copy):
+            pv_grouped[g] = work.tile(
+                [P, K_PASS, 4], BF16, tag="pv_grouped", name="pv_grouped", bufs=1, align_bytes=64
+            )
+            copy(out=pv_grouped[g][:], in_=pv_raw[g][:].rearrange("q j c -> q c j"))
+
+        def quantise_values(g):
+            cols = slice(K_PASS * g, K_PASS * (g + 1))
+            nc.vector.quantize_mx(
+                out=pv_codes[:, cols].bitcast(FP8X4),
+                scales=pv_scales[:, cols],
+                in_=pv_grouped[g][:].rearrange("q c j -> q (c j)"),
+            )
+
+        def row_max(i):
+            r, j = divmod(i, GROUP)
+            if j == 0:
+                shift[r] = stats.tile([P, GROUP], F32, tag="shift", name="shift")
+                rowsum[r] = stats.tile([P, GROUP], F32, tag="rowsum", name="rowsum")
+            scaled[i] = s_pool.tile([P, PROMPT], F32, tag="scaled", name="scaled")
+            nc.vector.tensor_scalar(
+                out=scaled[i][:],
+                in0=banks["score", i][:],
+                scalar1=-SCALE,
+                scalar2=None,
+                op0=ALU.mult,
+                op1=ALU.min,
+                accum_out=shift[r][:, j : j + 1],
+            )
+
+        def exponential(i):
+            r, j = divmod(i, GROUP)
+            e_sb[i] = e_pool.tile([P, PROMPT], BF16, tag="e_sb", name="e_sb")
+            nc.scalar.activation(
+                out=e_sb[i][:],
+                in_=scaled[i][:],
+                func=ACT.Exp,
+                bias=shift[r][:, j : j + 1],
+                scale=-1.0,
+                accum_out=rowsum[r][:, j : j + 1],
+            )
+
+        def empty_e(pair, copy):
+            r, half = divmod(pair, 2)
+            if half == 0:
+                e_grouped[r] = work.tile(
+                    [P, GROUP * P * 4], BF16, tag="e_grouped", name="e_grouped", align_bytes=64
+                )
+            e_words = e_grouped[r][:].bitcast(F32).rearrange("q (j m u) -> q j m u", j=GROUP, u=2)
+            copy(
+                out=e_words[:, 2 * half : 2 * half + 2, :, :],
+                in_=banks["e", pair][:].rearrange("q j u m -> q j m u"),
+            )
+
+        def divide_gate(r):
+            g = r % PASSES
+            weight[r] = stats.tile([P, GROUP], F32, tag="weight", name="weight")
+            nc.gpsimd.tensor_mul(
+                out=weight[r][:], in0=rowsum[r][:], in1=inverse_gate[:, GROUP * g : GROUP * (g + 1)]
+            )
+
+        def quantise_e(r):
+            e_codes[r] = work.tile([P, GROUP * P], U32, tag="e_codes", name="e_codes", align_bytes=64)
+            e_scales[r] = work.tile([P, GROUP * P], U8, tag="e_scales", name="e_scales", align_bytes=64)
+            nc.vector.quantize_mx(
+                out=e_codes[r][:].bitcast(FP8X4), scales=e_scales[r][:], in_=e_grouped[r][:]
+            )
+            nc.vector.reciprocal(out=weight[r][:], in_=weight[r][:])
+
+        def combine(r, heads):
+            rt, g = divmod(r, PASSES)
+            b, t = divmod(rt, 2)
+            if heads[0] == 0:
+                fused[r] = work.tile([P, K_PASS], BF16, tag="fused", name="fused", bufs=4)
+            for j in heads:
+                nc.vector.scalar_tensor_tensor(
+                    out=fused[r][:, HEAD_DIM * j : HEAD_DIM * (j + 1)],
+                    in0=num_ps[r][:, j, :],
+                    scalar=weight[r][:, j : j + 1],
+                    in1=ha_sb[:, b, GROUP * g + j, HEAD_DIM * t : HEAD_DIM * (t + 1)],
+                    op0=ALU.mult,
+                    op1=ALU.add,
+                )
+
+        def empty_fused(r):
+            n_rounds = len(fused_rounds(r))
+            f_grouped[r] = work.tile(
+                [P, n_rounds * P * 4], BF16, tag="f_grouped", name="f_grouped", align_bytes=64
+            )
+            nc.scalar.copy(
+                out=f_grouped[r][:].bitcast(F32).rearrange("q (n m u) -> q n m u", n=n_rounds, u=2),
+                in_=banks["fused", r][:].rearrange("q n u m -> q n m u"),
+            )
+
+        def quantise_fused(r):
+            cols = slice(P * fused_rounds(r)[0], P * (r + 1))
+            nc.vector.quantize_mx(
+                out=fused_codes[:, cols].bitcast(FP8X4), scales=fused_scales[:, cols], in_=f_grouped[r][:]
+            )
+
+        def store(piece, copy):
             rt, n = divmod(piece, N_TILES)
             b, t = divmod(rt, 2)
             result = results.tile([P, N_TILE], F32, tag="result")
-            if rt == ROW_TILES - 1 and n % 2 == 1:
-                nc.vector.tensor_copy(out=result[:], in_=acc[piece][:])
-            else:
-                nc.scalar.copy(out=result[:], in_=acc[piece][:])
+            copy(out=result[:], in_=acc[piece][:])
             nc.sync.dma_start(out=out_view[b, t][:, N_TILE * n : N_TILE * (n + 1)], in_=result[:])
 
-        e_flip = 1 + LAG
-        e_quant = GROUP - 1 + 2 * LAG
-        values = e_quant + LAG
-        f_flip = values + 1 + LAG
-        f_quant = f_flip + LAG
-        pieces_from = GROUP * (PASSES - 1) + f_quant + LAG
-        last_step = HEADS * (ROW_TILES - 1) + pieces_from + PIECE_EVERY * (N_TILES - 1)
+        on_vector, on_scalar = nc.vector.tensor_copy, nc.scalar.copy
+        ctx.enter_context(tc.manual_schedule())
 
         load_keys(0, 0, 2)
         load_queries(0, 0)
-        load_wo(0)
         load_keys(0, 2, GROUP)
-        load_values(0)
         load_keys(1, 0, GROUP)
         load_queries(0, 1)
-        load_wo(1)
-        load_attention(0, 0)
-        load_values(1)
-        load_attention(0, 1)
-        gate_bf = keep.tile([P, HEADS], BF16)
+        load_values(0)
         nc.sync.dma_start(
             out=gate_bf[:], in_=prompt_gate.rearrange("a h b c -> (a h b c)").partition_broadcast(P)
         )
-        inverse_gate = keep.tile([P, HEADS], F32)
+        load_wo(0)
+        load_keys(2, 0, GROUP)
+        load_queries(0, 2)
+        load_attention(0, 0)
+        load_values(1)
+        load_keys(3, 0, GROUP)
+        load_queries(0, 3)
+        load_attention(0, 1)
+        load_wo(1)
+        load_values(2)
+        load_attention(0, 2)
+        load_values(3)
+        load_attention(0, 3)
         flip_keys(0, 1)
-        flip_queries(0, [0], nc.scalar.copy)
+        flip_queries(0, 0, [0])
         flip_keys(1, 1)
+        empty_keys(0, 1, on_vector)
+        empty_queries(0, 0, [0], on_scalar)
+        empty_keys(1, 1, on_vector)
+        keys_out, queries_out, wo_out, e_out, f_out, piece_out = None, [], None, [], None, None
 
-        for i in range(last_step + 1):
-            ahead = due(i, -2 * GROUP, GROUP, WO_LOADS)
-            if ahead is not None and ahead >= 2:
-                if ahead < PASSES:
-                    load_keys(ahead, 0, GROUP)
-                    load_queries(0, ahead)
-                    load_values(ahead)
-                    load_attention(0, ahead)
-                load_wo(ahead)
-                if PASSES <= ahead < PASSES + 2:
-                    for g in (2 * (ahead - PASSES), 2 * (ahead - PASSES) + 1):
-                        load_queries(1, g)
-                        load_attention(1, g)
+        E_FLIP, E_QUANT, VALUES, COMBINE, F_FLIP, F_QUANT = LAGS
 
-            r_values = due(i, values, GROUP, ROUNDS)
-            if r_values is not None:
-                multiply_values(r_values)
-            piece = None
-            for rt in range(ROW_TILES):
-                n = due(i, HEADS * rt + pieces_from, PIECE_EVERY, N_TILES)
-                if n is not None:
-                    piece = N_TILES * rt + n
-            if piece is not None:
-                project(piece)
+        def soon(nominal, earliest):
+            return min(nominal, max(STEPS, earliest))
+
+        e_flip, e_quant, values, combines, f_flip, f_quant = {}, {}, {}, {}, {}, {}
+        for r in range(ROUNDS):
+            for p in (2 * r, 2 * r + 1):
+                fed = soon(2 * p + E_FLIP, 2 * p + 2 + EL)
+                e_flip[fed] = e_flip.get(fed, []) + [p]
+            fed = soon(GROUP * r + E_QUANT, fed + 2)
+            e_quant[fed] = r
+            fed = soon(GROUP * r + VALUES, fed + 1)
+            values[fed] = r
+            fed = soon(GROUP * r + COMBINE, fed)
+            combines[fed] = r
+            if fused_rounds(r):
+                fed = soon(GROUP * r + F_FLIP, fed + 1)
+                f_flip[fed] = r
+                fed = soon(GROUP * r + F_QUANT, fed + 2)
+                f_quant[fed] = r
+        fq_step = {r: s for s, r in f_quant.items()}
+        wo_steps = {wo_unit_step(unit): unit for unit in range(UNITS)}
+        wo_quants = {wo_unit_step(u) + WQ: u for u in range(UNITS)}
+        project_steps, step = {}, 0
+        for rt in range(ROW_TILES - 1):
+            for n in range(N_TILES):
+                step = max(fq_step[PASSES * rt + PASSES - 1] + 1, wo_unit_step(8 * n + 7) + WQ + 1, step + PEV)
+                project_steps[step] = N_TILES * rt + n
+        last_quant = fq_step[ROUNDS - 1]
+        last_row_tile = {}
+        for g in range(PASSES):
+            r = ROUNDS - PASSES + g
+            s = fq_step.get(r, fq_step.get(r + 1)) + 1
+            s = max(s, LPG[g] + last_quant)
+            last_row_tile[s] = last_row_tile.get(s, []) + [g]
+        for i in range(last_quant + 3):
+            if i in (12, 16, 20, 24):
+                load_queries(1, i // 4 - 3)
+                load_attention(1, i // 4 - 3)
+            for load in range(2, 8):
+                if i == WO_LOAD(load):
+                    load_wo(load)
+
             if i < STEPS:
                 score(i)
-            pair = due(i, e_flip, 2, STEPS // 2)
-            if pair is not None:
-                flip_e(pair)
-            r_fused = due(i, f_flip, GROUP, ROUNDS)
-            if r_fused is not None and fused_rounds(r_fused):
+            r_values = values.get(i)
+            if r_values is not None:
+                multiply_values(r_values)
+            piece = project_steps.get(i)
+            if piece is not None and i < STEPS:
+                project(piece, range(PASSES))
+            pair = e_flip.get(i, [])
+            for one in pair:
+                flip_e(one)
+            r_fused = f_flip.get(i)
+            if r_fused is not None:
                 flip_fused(r_fused)
+            keys = i + 2 if i % 2 == 0 and i + 2 < HEADS else None
+            if keys is not None:
+                flip_keys(keys, 2)
+            queries = []
             for b in range(BATCH):
-                g_next = due(i, 2 * HEADS * b - GROUP, GROUP, PASSES)
-                if g_next is not None and (b > 0 or g_next >= 1):
-                    flip_queries(PASSES * b + g_next, [0, 1], nc.vector.tensor_copy)
-            if i == 2:
-                flip_queries(0, [1], nc.vector.tensor_copy)
-            if i % 2 == 0 and i + 2 < HEADS:
-                flip_keys(i + 2, 2)
-            if i < UNITS:
-                flip_wo(i)
+                g = due(i, 2 * HEADS * b - QPH, GROUP, PASSES)
+                if g is not None:
+                    queries.append((b, g, [0, 1]))
+            if i == 5:
+                queries.append((0, 0, [1]))
+            for one in queries:
+                flip_queries(*one)
+            unit = wo_steps.get(i)
+            if unit is not None:
+                flip_wo(unit)
+            if piece is not None and i >= STEPS:
+                project(piece, range(PASSES))
+            last = last_row_tile.get(i)
+            if last:
+                for n in range(N_TILES):
+                    project(N_TILES * (ROW_TILES - 1) + n, last)
 
-            for half in range(2):
-                r_comb = due(i, values + half, GROUP, ROUNDS)
-                if r_comb is not None:
-                    combine(r_comb, half)
-            r_e = due(i, e_quant, GROUP, ROUNDS)
+            if i < STEPS and MAXFIRST:
+                row_max(i)
+            g = due(i, PVQ, GROUP, PASSES)
+            if g is not None:
+                quantise_values(g)
+            if i == 4:
+                nc.vector.reciprocal(out=inverse_gate[:], in_=gate_bf[:])
+            r_e = e_quant.get(i)
             if r_e is not None:
-                if r_e == 0:
-                    nc.vector.reciprocal(out=inverse_gate[:], in_=gate_bf[:])
                 quantise_e(r_e)
-            r_q = due(i, f_quant, GROUP, ROUNDS)
-            if r_q is not None and fused_rounds(r_q):
+            r_comb = combines.get(i)
+            if r_comb is not None:
+                combine(r_comb, range(GROUP))
+            r_q = f_quant.get(i)
+            if r_q is not None:
                 quantise_fused(r_q)
-            tile = due(i, 2, 2, UNITS // 2)
-            if tile is not None:
-                quantise_wo(tile)
-            g_group = due(i, 2, GROUP, PASSES)
-            if g_group is not None:
-                group_values(g_group)
-            g_quant = due(i, GROUP, GROUP, PASSES)
-            if g_quant is not None:
-                quantise_values(g_quant)
-            if piece is not None:
-                store(piece)
+            u = wo_quants.get(i)
+            if u is not None:
+                quantise_wo(u)
+            if i < STEPS and not MAXFIRST and not MAXLAST:
+                row_max(i)
+            if keys_out is not None and not KEYS_ON_SCALAR(keys_out):
+                empty_keys(keys_out, 2, on_vector)
+            if not Q_ON_SCALAR:
+                for one in queries_out:
+                    empty_queries(*one, on_vector)
+            if wo_out is not None and WO_ON_VECTOR(wo_out):
+                empty_wo(wo_out, on_vector)
+            g = due(i, PVG, GROUP, PASSES)
+            if g is not None and not PV_ON_SCALAR(g):
+                group_values(g, on_vector)
+            if piece_out is not None and OUT_ON_VECTOR(piece_out):
+                store(piece_out, on_vector)
+            if i < STEPS and MAXLAST:
+                row_max(i)
+
+            if EL <= i < STEPS + EL and i >= STEPS - 1:
+                exponential(i - EL)
+                if (i - EL) % GROUP == GROUP - 1:
+                    divide_gate((i - EL) // GROUP)
+            for one in e_out:
+                empty_e(one, on_scalar)
+            if keys_out is not None and KEYS_ON_SCALAR(keys_out):
+                empty_keys(keys_out, 2, on_scalar)
+            if Q_ON_SCALAR:
+                for one in queries_out:
+                    empty_queries(*one, on_scalar)
+            if f_out is not None:
+                empty_fused(f_out)
+            if EL <= i < STEPS - 1:
+                exponential(i - EL)
+                if (i - EL) % GROUP == GROUP - 1:
+                    divide_gate((i - EL) // GROUP)
+            if wo_out is not None and not WO_ON_VECTOR(wo_out):
+                empty_wo(wo_out, on_scalar)
+            if g is not None and PV_ON_SCALAR(g):
+                group_values(g, on_scalar)
+            if piece_out is not None and not OUT_ON_VECTOR(piece_out):
+                store(piece_out, on_scalar)
+            if i == last_quant + 2:
+                for n in range(N_TILES):
+                    store(N_TILES * (ROW_TILES - 1) + n, on_vector if n % 2 else on_scalar)
+            keys_out, queries_out, wo_out, e_out, f_out, piece_out = keys, queries, unit, pair, r_fused, piece

@@ -33,7 +33,10 @@ PVG = 3
 MAXFIRST = False
 MAXLAST = False
 EXPFIRST = False
-Q_ON_SCALAR = False
+
+
+def Q_ON_SCALAR(one):
+    return one[0] == 0
 
 
 def WO_STEP(u):
@@ -52,12 +55,12 @@ def KEYS_ON_SCALAR(i):
     return True
 
 
-def WO_ON_VECTOR(unit):
-    return False
+def WO_ON_VECTOR(u):
+    return u % 8 == 7 and 8 <= u < 24
 
 
-def OUT_ON_VECTOR(piece):
-    return False
+def OUT_ON_VECTOR(p):
+    return p >= 8 and p % 2 == 1
 
 
 EL = 2
@@ -65,7 +68,7 @@ EPB = 9
 WQ = 3
 WOB = 6
 WRB = 3
-LPG = (-3, -2, 0, 1)
+LPG = (-4, -3, -1, 1)
 STEPS = ROW_TILES * HEADS
 ROUNDS = STEPS // GROUP
 UNITS = D_OUT // BANK_ROWS * PASSES
@@ -279,7 +282,10 @@ def tile_attention_pb_kernel(tc, q_rot, pk, pv, prompt_gate, h_attn, wo, out):
             pv_grouped[g] = work.tile(
                 [P, K_PASS, 4], BF16, tag="pv_grouped", name="pv_grouped", bufs=1, align_bytes=64
             )
-            copy(out=pv_grouped[g][:], in_=pv_raw[g][:].rearrange("q j c -> q c j"))
+            copy(
+                out=pv_grouped[g][:].rearrange("q (c i) j -> q c j i", i=4),
+                in_=pv_raw[g][:].rearrange("q j (c i) -> q c j i", i=4),
+            )
 
         def quantise_values(g):
             cols = slice(K_PASS * g, K_PASS * (g + 1))
@@ -518,8 +524,8 @@ def tile_attention_pb_kernel(tc, q_rot, pk, pv, prompt_gate, h_attn, wo, out):
                 row_max(i)
             if keys_out is not None and not KEYS_ON_SCALAR(keys_out):
                 empty_keys(keys_out, 2, on_vector)
-            if not Q_ON_SCALAR:
-                for one in queries_out:
+            for one in queries_out:
+                if not Q_ON_SCALAR(one):
                     empty_queries(*one, on_vector)
             if wo_out is not None and WO_ON_VECTOR(wo_out):
                 empty_wo(wo_out, on_vector)
@@ -539,8 +545,8 @@ def tile_attention_pb_kernel(tc, q_rot, pk, pv, prompt_gate, h_attn, wo, out):
                 empty_e(one, on_scalar)
             if keys_out is not None and KEYS_ON_SCALAR(keys_out):
                 empty_keys(keys_out, 2, on_scalar)
-            if Q_ON_SCALAR:
-                for one in queries_out:
+            for one in queries_out:
+                if Q_ON_SCALAR(one):
                     empty_queries(*one, on_scalar)
             if f_out is not None:
                 empty_fused(f_out)

@@ -24,7 +24,7 @@ N_TILES = D_OUT // N_TILE
 BANK_ROWS = 2 * P
 SCALE = 1.0 / math.sqrt(HEAD_DIM)
 
-LAGS = (6, 10, 11, 13, 14, 16)
+LAGS = (6, 11, 12, 14, 15, 17)
 SINGLES = 4
 PEV = 2
 QPH = 3
@@ -63,12 +63,27 @@ def OUT_ON_VECTOR(p):
     return p >= 8 and p % 2 == 1
 
 
-EL = 2
-EPB = 9
+def E_ON_VECTOR(p):
+    return False
+
+
+EARLY = ()
+VLAST = False
 WQ = 3
 WOB = 6
 WRB = 3
 LPG = (-4, -3, -1, 1)
+LFROM = 11
+LAGS2 = (6, 10, 11, 13, 14, 16)
+
+
+def KEY_STEP(h):
+    return h - 2 if h <= 4 else h - 3
+
+
+KEYV1 = True
+EL = 2
+EPB = 9
 STEPS = ROW_TILES * HEADS
 ROUNDS = STEPS // GROUP
 UNITS = D_OUT // BANK_ROWS * PASSES
@@ -421,13 +436,13 @@ def tile_attention_pb_kernel(tc, q_rot, pk, pv, prompt_gate, h_attn, wo, out):
         empty_keys(1, 1, on_vector)
         keys_out, queries_out, wo_out, e_out, f_out, piece_out = None, [], None, [], None, None
 
-        E_FLIP, E_QUANT, VALUES, COMBINE, F_FLIP, F_QUANT = LAGS
 
         def soon(nominal, earliest):
             return min(nominal, max(STEPS, earliest))
 
         e_flip, e_quant, values, combines, f_flip, f_quant = {}, {}, {}, {}, {}, {}
         for r in range(ROUNDS):
+            E_FLIP, E_QUANT, VALUES, COMBINE, F_FLIP, F_QUANT = LAGS if r < LFROM else LAGS2
             for p in (2 * r, 2 * r + 1):
                 fed = soon(2 * p + E_FLIP, 2 * p + 2 + EL)
                 e_flip[fed] = e_flip.get(fed, []) + [p]
@@ -443,6 +458,7 @@ def tile_attention_pb_kernel(tc, q_rot, pk, pv, prompt_gate, h_attn, wo, out):
                 fed = soon(GROUP * r + F_QUANT, fed + 2)
                 f_quant[fed] = r
         fq_step = {r: s for s, r in f_quant.items()}
+        key_steps = {KEY_STEP(h): h for h in range(2, HEADS, 2)}
         wo_steps = {wo_unit_step(unit): unit for unit in range(UNITS)}
         wo_quants = {wo_unit_step(u) + WQ: u for u in range(UNITS)}
         project_steps, step = {}, 0
@@ -467,9 +483,6 @@ def tile_attention_pb_kernel(tc, q_rot, pk, pv, prompt_gate, h_attn, wo, out):
 
             if i < STEPS:
                 score(i)
-            r_values = values.get(i)
-            if r_values is not None:
-                multiply_values(r_values)
             piece = project_steps.get(i)
             if piece is not None and i < STEPS:
                 project(piece, range(PASSES))
@@ -479,7 +492,7 @@ def tile_attention_pb_kernel(tc, q_rot, pk, pv, prompt_gate, h_attn, wo, out):
             r_fused = f_flip.get(i)
             if r_fused is not None:
                 flip_fused(r_fused)
-            keys = i + 2 if i % 2 == 0 and i + 2 < HEADS else None
+            keys = key_steps.get(i)
             if keys is not None:
                 flip_keys(keys, 2)
             queries = []
@@ -492,7 +505,12 @@ def tile_attention_pb_kernel(tc, q_rot, pk, pv, prompt_gate, h_attn, wo, out):
             for one in queries:
                 flip_queries(*one)
             unit = wo_steps.get(i)
-            if unit is not None:
+            if unit is not None and not VLAST:
+                flip_wo(unit)
+            r_values = values.get(i)
+            if r_values is not None:
+                multiply_values(r_values)
+            if unit is not None and VLAST:
                 flip_wo(unit)
             if piece is not None and i >= STEPS:
                 project(piece, range(PASSES))
@@ -503,10 +521,12 @@ def tile_attention_pb_kernel(tc, q_rot, pk, pv, prompt_gate, h_attn, wo, out):
 
             if i < STEPS and MAXFIRST:
                 row_max(i)
+            if keys_out is not None and not KEYS_ON_SCALAR(keys_out) and KEYV1:
+                empty_keys(keys_out, 2, on_vector)
             g = due(i, PVQ, GROUP, PASSES)
             if g is not None:
                 quantise_values(g)
-            if i == 4:
+            if i == 5:
                 nc.vector.reciprocal(out=inverse_gate[:], in_=gate_bf[:])
             r_e = e_quant.get(i)
             if r_e is not None:
@@ -522,13 +542,16 @@ def tile_attention_pb_kernel(tc, q_rot, pk, pv, prompt_gate, h_attn, wo, out):
                 quantise_wo(u)
             if i < STEPS and not MAXFIRST and not MAXLAST:
                 row_max(i)
-            if keys_out is not None and not KEYS_ON_SCALAR(keys_out):
+            if keys_out is not None and not KEYS_ON_SCALAR(keys_out) and not KEYV1:
                 empty_keys(keys_out, 2, on_vector)
             for one in queries_out:
                 if not Q_ON_SCALAR(one):
                     empty_queries(*one, on_vector)
             if wo_out is not None and WO_ON_VECTOR(wo_out):
                 empty_wo(wo_out, on_vector)
+            for one in e_out:
+                if E_ON_VECTOR(one):
+                    empty_e(one, on_vector)
             g = due(i, PVG, GROUP, PASSES)
             if g is not None and not PV_ON_SCALAR(g):
                 group_values(g, on_vector)
@@ -542,7 +565,8 @@ def tile_attention_pb_kernel(tc, q_rot, pk, pv, prompt_gate, h_attn, wo, out):
                 if (i - EL) % GROUP == GROUP - 1:
                     divide_gate((i - EL) // GROUP)
             for one in e_out:
-                empty_e(one, on_scalar)
+                if not E_ON_VECTOR(one):
+                    empty_e(one, on_scalar)
             if keys_out is not None and KEYS_ON_SCALAR(keys_out):
                 empty_keys(keys_out, 2, on_scalar)
             for one in queries_out:
@@ -550,7 +574,9 @@ def tile_attention_pb_kernel(tc, q_rot, pk, pv, prompt_gate, h_attn, wo, out):
                     empty_queries(*one, on_scalar)
             if f_out is not None:
                 empty_fused(f_out)
-            if EL <= i < STEPS - 1:
+            if i in EARLY:
+                exponential(i - 1)
+            if EL <= i < STEPS - 1 and i - EL not in [k - 1 for k in EARLY]:
                 exponential(i - EL)
                 if (i - EL) % GROUP == GROUP - 1:
                     divide_gate((i - EL) // GROUP)

@@ -27,7 +27,7 @@ SCALE = 1.0 / math.sqrt(HEAD_DIM)
 LAGS = (6, 11, 12, 14, 15, 17)
 SINGLES = 4
 PEV = 2
-QPH = 3
+QPH = (3, 5)
 PVQ = 5
 PVG = 3
 MAXFIRST = False
@@ -64,7 +64,7 @@ def OUT_ON_VECTOR(p):
 
 
 def E_ON_VECTOR(p):
-    return False
+    return p % 8 == 1 and p >= 16
 
 
 EARLY = ()
@@ -84,6 +84,7 @@ def KEY_STEP(h):
 KEYV1 = True
 EL = 2
 EPB = 9
+DFROM = 32
 STEPS = ROW_TILES * HEADS
 ROUNDS = STEPS // GROUP
 UNITS = D_OUT // BANK_ROWS * PASSES
@@ -144,7 +145,7 @@ def tile_attention_pb_kernel(tc, q_rot, pk, pv, prompt_gate, h_attn, wo, out):
         inverse_gate = keep.tile([P, HEADS], F32)
 
         q_raw, pk_raw, pv_raw, wo_raw, pv_grouped, wo_grouped = {}, {}, {}, {}, {}, {}
-        banks, qT, scaled, shift, rowsum, weight = {}, {}, {}, {}, {}, {}
+        banks, qT, peak, scaled, shift, rowsum, weight = {}, {}, {}, {}, {}, {}, {}
         e_sb, e_grouped, e_codes, e_scales, num_ps, fused, f_grouped, acc = {}, {}, {}, {}, {}, {}, {}, {}
 
         def load_queries(b, g):
@@ -313,8 +314,22 @@ def tile_attention_pb_kernel(tc, q_rot, pk, pv, prompt_gate, h_attn, wo, out):
         def row_max(i):
             r, j = divmod(i, GROUP)
             if j == 0:
+                peak[r] = stats.tile([P, GROUP], F32, tag="peak", name="peak")
                 shift[r] = stats.tile([P, GROUP], F32, tag="shift", name="shift")
                 rowsum[r] = stats.tile([P, GROUP], F32, tag="rowsum", name="rowsum")
+            if i >= DFROM:
+                nc.vector.tensor_reduce(
+                    out=peak[r][:, j : j + 1], in_=banks["score", i][:], axis=mybir.AxisListType.X, op=ALU.max
+                )
+                nc.gpsimd.tensor_scalar(
+                    out=shift[r][:, j : j + 1],
+                    in0=peak[r][:, j : j + 1],
+                    scalar1=-SCALE,
+                    scalar2=0.0,
+                    op0=ALU.mult,
+                    op1=ALU.add,
+                )
+                return
             scaled[i] = s_pool.tile([P, PROMPT], F32, tag="scaled", name="scaled")
             nc.vector.tensor_scalar(
                 out=scaled[i][:],
@@ -331,10 +346,10 @@ def tile_attention_pb_kernel(tc, q_rot, pk, pv, prompt_gate, h_attn, wo, out):
             e_sb[i] = e_pool.tile([P, PROMPT], BF16, tag="e_sb", name="e_sb")
             nc.scalar.activation(
                 out=e_sb[i][:],
-                in_=scaled[i][:],
+                in_=banks["score", i][:] if i >= DFROM else scaled[i][:],
                 func=ACT.Exp,
                 bias=shift[r][:, j : j + 1],
-                scale=-1.0,
+                scale=SCALE if i >= DFROM else -1.0,
                 accum_out=rowsum[r][:, j : j + 1],
             )
 
@@ -497,7 +512,7 @@ def tile_attention_pb_kernel(tc, q_rot, pk, pv, prompt_gate, h_attn, wo, out):
                 flip_keys(keys, 2)
             queries = []
             for b in range(BATCH):
-                g = due(i, 2 * HEADS * b - QPH, GROUP, PASSES)
+                g = due(i, 2 * HEADS * b - QPH[b], GROUP, PASSES)
                 if g is not None:
                     queries.append((b, g, [0, 1]))
             if i == 5:

@@ -24,7 +24,7 @@ N_TILES = D_OUT // N_TILE
 BANK_ROWS = 2 * P
 SCALE = 1.0 / math.sqrt(HEAD_DIM)
 
-LAGS = (6, 11, 12, 14, 15, 17)
+LAGS = (5, 11, 12, 14, 15, 17)
 SINGLES = 4
 PEV = 2
 QPH = (3, 5)
@@ -123,7 +123,7 @@ def tile_attention_pb_kernel(tc, q_rot, pk, pv, prompt_gate, h_attn, wo, out):
         work = ctx.enter_context(tc.tile_pool(name="work", bufs=3))
         e_pool = ctx.enter_context(tc.tile_pool(name="e_pool", bufs=EPB))
         stats = ctx.enter_context(tc.tile_pool(name="stats", bufs=6))
-        s_pool = ctx.enter_context(tc.tile_pool(name="s_pool", bufs=4))
+        s_pool = ctx.enter_context(tc.tile_pool(name="s_pool", bufs=7))
         results = ctx.enter_context(tc.tile_pool(name="results", bufs=4))
         psum_any = ctx.enter_context(tc.psum_pool(name="psum_any", bufs=7))
         psum_num = ctx.enter_context(tc.psum_pool(name="psum_num", bufs=1))
@@ -421,9 +421,8 @@ def tile_attention_pb_kernel(tc, q_rot, pk, pv, prompt_gate, h_attn, wo, out):
         on_vector, on_scalar = nc.vector.tensor_copy, nc.scalar.copy
         ctx.enter_context(tc.manual_schedule())
 
-        load_keys(0, 0, 2)
+        load_keys(0, 0, GROUP)
         load_queries(0, 0)
-        load_keys(0, 2, GROUP)
         load_keys(1, 0, GROUP)
         load_queries(0, 1)
         load_values(0)
@@ -433,15 +432,15 @@ def tile_attention_pb_kernel(tc, q_rot, pk, pv, prompt_gate, h_attn, wo, out):
         load_wo(0)
         load_keys(2, 0, GROUP)
         load_queries(0, 2)
-        load_attention(0, 0)
         load_values(1)
         load_keys(3, 0, GROUP)
         load_queries(0, 3)
-        load_attention(0, 1)
         load_wo(1)
+        load_attention(0, 0)
         load_values(2)
-        load_attention(0, 2)
+        load_attention(0, 1)
         load_values(3)
+        load_attention(0, 2)
         load_attention(0, 3)
         flip_keys(0, 1)
         flip_queries(0, 0, [0])

@@ -64,7 +64,7 @@ def OUT_ON_VECTOR(p):
 
 
 def E_ON_VECTOR(p):
-    return p % 8 == 1 and p >= 16
+    return p % 8 == 1 and p >= 24
 
 
 EARLY = ()
@@ -115,7 +115,7 @@ def tile_attention_pb_kernel(tc, q_rot, pk, pv, prompt_gate, h_attn, wo, out):
     out_view = out.rearrange("b (m t) n -> b t m n", t=2)
     pk_view = pk.rearrange("(c p) h d -> p c (h d)", p=P)
     pv_view = pv.rearrange("(u q e) h d -> u q e (h d)", u=2, e=2)
-    wo_view = wo.rearrange("(n p) k -> p n k", p=P)
+    wo_view = wo.rearrange("(c p n) k -> c p n k", p=P, n=2)
 
     with ExitStack() as ctx:
         keep = ctx.enter_context(tc.tile_pool(name="keep", bufs=1))
@@ -172,7 +172,7 @@ def tile_attention_pb_kernel(tc, q_rot, pk, pv, prompt_gate, h_attn, wo, out):
 
         def load_wo(load):
             wo_raw[load] = raw.tile([P, 2, K_FUSED], BF16, tag="wo_raw", name="wo_raw", bufs=WRB)
-            nc.sync.dma_start(out=wo_raw[load][:], in_=wo_view[:, 2 * load : 2 * load + 2, :])
+            nc.sync.dma_start(out=wo_raw[load][:], in_=wo_view[load])
 
         def flip_keys(h, heads):
             g, j = divmod(h, GROUP)
@@ -281,8 +281,8 @@ def tile_attention_pb_kernel(tc, q_rot, pk, pv, prompt_gate, h_attn, wo, out):
                 [P, 4 * BANK_ROWS], BF16, tag="wo_grouped", name="wo_grouped", bufs=WOB, align_bytes=64
             )
             copy(
-                out=wo_grouped[unit][:].bitcast(F32).rearrange("q (n p u) -> q n p u", n=2, u=2),
-                in_=banks["wo", unit][:].rearrange("q n u p -> q n p u"),
+                out=wo_grouped[unit][:].bitcast(F32).rearrange("q (p n u) -> q p n u", n=2, u=2),
+                in_=banks["wo", unit][:].rearrange("q n u p -> q p n u"),
             )
 
         def quantise_wo(unit):
@@ -436,8 +436,8 @@ def tile_attention_pb_kernel(tc, q_rot, pk, pv, prompt_gate, h_attn, wo, out):
         load_keys(3, 0, GROUP)
         load_queries(0, 3)
         load_wo(1)
-        load_attention(0, 0)
         load_values(2)
+        load_attention(0, 0)
         load_attention(0, 1)
         load_values(3)
         load_attention(0, 2)

import math
from contextlib import ExitStack

import concourse.mybir as mybir
from concourse.masks import make_identity

F32 = mybir.dt.float32
BF16 = mybir.dt.bfloat16
U32 = mybir.dt.uint32
U8 = mybir.dt.uint8
FP8X4 = mybir.dt.float8_e4m3fn_x4
ACT = mybir.ActivationFunctionType
ALU = mybir.AluOpType

P = 128
BATCH, HEADS, SEQ, HEAD_DIM, PROMPT, D_OUT = 2, 16, 256, 128, 512, 2048
K_FUSED = HEADS * HEAD_DIM
K_PASS = 4 * P
PASSES = K_FUSED // K_PASS
GROUP = K_PASS // HEAD_DIM
ROW_TILES = BATCH * SEQ // P
N_TILE = 512
N_TILES = D_OUT // N_TILE
BANK_ROWS = 2 * P
SCALE = 1.0 / math.sqrt(HEAD_DIM)

LAGS = (5, 11, 12, 14, 15, 17)
SINGLES = 4
PEV = 2
QPH = (3, 5)
PVQ = 5
PVG = 3
MAXFIRST = False
MAXLAST = False
EXPFIRST = False


def Q_ON_SCALAR(one):
    return one[0] == 0


def WO_STEP(u):
    return 2 * u + 3 if u < 8 else 18 + u - 8 if u < 20 else 30 + (4 * (u - 20) + 2) // 3


def WO_LOAD(l):
    return max(1, WO_STEP(4 * l) - 9)


def PV_ON_SCALAR(g):
    return False


def KEYS_ON_SCALAR(i):
    return True


def WO_ON_VECTOR(u):
    return u % 8 == 7 and 8 <= u < 24


def OUT_ON_VECTOR(p):
    return p >= 8 and p % 2 == 1


def E_ON_VECTOR(p):
    return p % 8 == 1 and p >= 24


EARLY = ()
VLAST = False
WQ = 3
WOB = 6
WRB = 3
LPG = (-4, -3, -1, 1)
LFROM = 11
LAGS2 = (6, 10, 11, 13, 14, 16)


def KEY_STEP(h):
    return h - 2 if h <= 4 else h - 3


KEYV1 = True
EL = 2
EPB = 9
DFROM = 32
STEPS = ROW_TILES * HEADS
ROUNDS = STEPS // GROUP
UNITS = D_OUT // BANK_ROWS * PASSES

FLOPS = 2 * (2 * BATCH * HEADS * SEQ * HEAD_DIM * PROMPT) + 2 * BATCH * SEQ * K_FUSED * D_OUT


def due(step, first, every, count):
    k, rest = divmod(step - first, every)
    return k if rest == 0 and 0 <= k < count else None


def fused_rounds(r):
    if r >= ROUNDS - SINGLES:
        return [r]
    return [r - 1, r] if r % 2 == 1 else []


def wo_unit_step(unit):
    return WO_STEP(unit)


def tile_attention_pb_kernel(tc, q_rot, pk, pv, prompt_gate, h_attn, wo, out):
    nc = tc.nc

    q_view = q_rot.rearrange("b h (m t) d -> b m h (t d)", t=2)
    ha_view = h_attn.rearrange("b h (m t) d -> b m h (t d)", t=2)
    out_view = out.rearrange("b (m t) n -> b t m n", t=2)
    pk_view = pk.rearrange("(c p) h d -> p c (h d)", p=P)
    pv_view = pv.rearrange("(u q e) h d -> u q e (h d)", u=2, e=2)
    wo_view = wo.rearrange("(c p n) k -> c p n k", p=P, n=2)

    with ExitStack() as ctx:
        keep = ctx.enter_context(tc.tile_pool(name="keep", bufs=1))
        raw = ctx.enter_context(tc.tile_pool(name="raw", bufs=3))
        work = ctx.enter_context(tc.tile_pool(name="work", bufs=3))
        e_pool = ctx.enter_context(tc.tile_pool(name="e_pool", bufs=EPB))
        stats = ctx.enter_context(tc.tile_pool(name="stats", bufs=6))
        s_pool = ctx.enter_context(tc.tile_pool(name="s_pool", bufs=7))
        results = ctx.enter_context(tc.tile_pool(name="results", bufs=4))
        psum_any = ctx.enter_context(tc.psum_pool(name="psum_any", bufs=7))
        psum_num = ctx.enter_context(tc.psum_pool(name="psum_num", bufs=1))

        ident_bf = keep.tile([P, P], BF16)
        make_identity(nc, ident_bf[:])
        ident_f32 = keep.tile([P, P], F32)
        make_identity(nc, ident_f32[:])

        ha_sb = keep.tile([P, BATCH, HEADS, 2 * HEAD_DIM], BF16)
        pkT = keep.tile([P, HEADS, PROMPT], BF16)
        pv_codes = keep.tile([P, K_FUSED], U32, align_bytes=64)
        pv_scales = keep.tile([P, K_FUSED], U8, align_bytes=64)
        wo_codes = keep.tile([P, PASSES, D_OUT], U32, align_bytes=64)
        wo_scales = keep.tile([P, PASSES, D_OUT], U8, align_bytes=64)
        fused_codes = keep.tile([P, ROUNDS * P], U32, align_bytes=64)
        fused_scales = keep.tile([P, ROUNDS * P], U8, align_bytes=64)
        gate_bf = keep.tile([P, HEADS], BF16)
        inverse_gate = keep.tile([P, HEADS], F32)

        q_raw, pk_raw, pv_raw, wo_raw, pv_grouped, wo_grouped = {}, {}, {}, {}, {}, {}
        banks, qT, peak, scaled, shift, rowsum, weight = {}, {}, {}, {}, {}, {}, {}
        e_sb, e_grouped, e_codes, e_scales, num_ps, fused, f_grouped, acc = {}, {}, {}, {}, {}, {}, {}, {}

        def load_queries(b, g):
            heads = slice(GROUP * g, GROUP * (g + 1))
            q_raw[b, g] = raw.tile([P, GROUP, 2 * HEAD_DIM], BF16, tag="q_raw", name="q_raw", bufs=4)
            nc.sync.dma_start(out=q_raw[b, g][:], in_=q_view[b][:, heads, :])

        def load_attention(b, g):
            heads = slice(GROUP * g, GROUP * (g + 1))
            nc.sync.dma_start(out=ha_sb[:, b, heads, :], in_=ha_view[b][:, heads, :])

        def load_keys(g, first, last):
            if first == 0:
                pk_raw[g] = raw.tile([P, PROMPT // P, K_PASS], BF16, tag="pk_raw", name="pk_raw")
            cols = slice(HEAD_DIM * first, HEAD_DIM * last)
            heads = slice(K_PASS * g + HEAD_DIM * first, K_PASS * g + HEAD_DIM * last)
            nc.sync.dma_start(out=pk_raw[g][:, :, cols], in_=pk_view[:, :, heads])

        def load_values(g):
            cols = slice(K_PASS * g, K_PASS * (g + 1))
            pv_raw[g] = raw.tile([P, 4, K_PASS], BF16, tag="pv_raw", name="pv_raw")
            for u in range(2):
                nc.sync.dma_start(out=pv_raw[g][:, 2 * u : 2 * u + 2, :], in_=pv_view[u][:, :, cols])

        def load_wo(load):
            wo_raw[load] = raw.tile([P, 2, K_FUSED], BF16, tag="wo_raw", name="wo_raw", bufs=WRB)
            nc.sync.dma_start(out=wo_raw[load][:], in_=wo_view[load])

        def flip_keys(h, heads):
            g, j = divmod(h, GROUP)
            banks["keys", h] = psum_any.tile([P, heads, PROMPT // P, P], BF16, tag="bank", name="pkT_ps")
            for n in range(heads):
                for c in range(PROMPT // P):
                    nc.tensor.transpose(
                        banks["keys", h][:, n, c, :],
                        pk_raw[g][:, c, HEAD_DIM * (j + n) : HEAD_DIM * (j + n + 1)],
                        ident_bf[:],
                    )

        def flip_queries(b, g, tiles):
            banks["queries", b, g, tiles[0]] = psum_any.tile(
                [P, len(tiles), GROUP, P], BF16, tag="bank", name="qT_ps"
            )
            for t in tiles:
                for j in range(GROUP):
                    nc.tensor.transpose(
                        banks["queries", b, g, tiles[0]][:, t - tiles[0], j, :],
                        q_raw[b, g][:, j, HEAD_DIM * t : HEAD_DIM * (t + 1)],
                        ident_bf[:],
                    )

        def flip_wo(unit):
            chunk, g = divmod(unit, PASSES)
            banks["wo", unit] = psum_any.tile([P, 2, 2, P], F32, tag="bank", name="woT_ps")
            for n in range(2):
                words = wo_raw[chunk][:, n, :].bitcast(F32)
                for u in range(2):
                    first = (K_PASS * g + 2 * P * u) // 2
                    nc.tensor.transpose(
                        banks["wo", unit][:, n, u, :], words[:, first : first + P], ident_f32[:]
                    )

        def score(i):
            r, j = divmod(i, GROUP)
            rt, g = divmod(r, PASSES)
            b, t = divmod(rt, 2)
            banks["score", i] = psum_any.tile([P, PROMPT], F32, tag="bank", name="score_ps")
            nc.tensor.matmul(
                banks["score", i][:], lhsT=qT[b, g][:, t, j, :], rhs=pkT[:, i % HEADS, :], start=True, stop=True
            )

        def flip_e(pair):
            banks["e", pair] = psum_any.tile([P, 2, 2, P], F32, tag="bank", name="eT_ps")
            for j in range(2):
                words = e_sb[2 * pair + j][:].bitcast(F32)
                for u in range(2):
                    nc.tensor.transpose(banks["e", pair][:, j, u, :], words[:, P * u : P * (u + 1)], ident_f32[:])

        def flip_fused(r):
            rounds = fused_rounds(r)
            banks["fused", r] = psum_any.tile([P, len(rounds), 2, P], F32, tag="bank", name="fT_ps")
            for n, one in enumerate(rounds):
                for u in range(2):
                    nc.tensor.transpose(
                        banks["fused", r][:, n, u, :],
                        fused[one][:].bitcast(F32)[:, P * u : P * (u + 1)],
                        ident_f32[:],
                    )

        def multiply_values(r):
            g = r % PASSES
            num_ps[r] = psum_num.tile([P, GROUP, HEAD_DIM], F32, tag="num", name="num_ps")
            for j in range(GROUP):
                e_cols = slice(P * j, P * (j + 1))
                v_cols = slice(HEAD_DIM * (GROUP * g + j), HEAD_DIM * (GROUP * g + j + 1))
                nc.tensor.matmul_mx(
                    out=num_ps[r][:, j, :],
                    lhsT=e_codes[r][:, e_cols].bitcast(FP8X4),
                    lhsT_scale=e_scales[r][:, e_cols],
                    rhs=pv_codes[:, v_cols].bitcast(FP8X4),
                    rhs_scale=pv_scales[:, v_cols],
                    start=True,
                    stop=True,
                )

        def project(piece, passes):
            rt, n = divmod(piece, N_TILES)
            cols = slice(N_TILE * n, N_TILE * (n + 1))
            if passes[0] == 0:
                acc[piece] = psum_any.tile([P, N_TILE], F32, tag="bank", name="acc")
            for g in passes:
                f_cols = slice(P * (PASSES * rt + g), P * (PASSES * rt + g + 1))
                nc.tensor.matmul_mx(
                    out=acc[piece][:],
                    lhsT=fused_codes[:, f_cols].bitcast(FP8X4),
                    lhsT_scale=fused_scales[:, f_cols],
                    rhs=wo_codes[:, g, cols].bitcast(FP8X4),
                    rhs_scale=wo_scales[:, g, cols],
                    start=(g == 0),
                    stop=(g == PASSES - 1),
                )

        def empty_keys(h, heads, copy):
            copy(out=pkT[:, h : h + heads, :], in_=banks["keys", h][:].rearrange("d n c p -> d n (c p)"))

        def empty_queries(b, g, tiles, copy):
            if tiles[0] == 0:
                qT[b, g] = raw.tile([P, 2, GROUP, P], BF16, tag="qT", name="qT", bufs=6)
            copy(out=qT[b, g][:, tiles[0] : tiles[0] + len(tiles), :, :], in_=banks["queries", b, g, tiles[0]][:])

        def empty_wo(unit, copy):
            wo_grouped[unit] = work.tile(
                [P, 4 * BANK_ROWS], BF16, tag="wo_grouped", name="wo_grouped", bufs=WOB, align_bytes=64
            )
            copy(
                out=wo_grouped[unit][:].bitcast(F32).rearrange("q (p n u) -> q p n u", n=2, u=2),
                in_=banks["wo", unit][:].rearrange("q n u p -> q p n u"),
            )

        def quantise_wo(unit):
            chunk, g = divmod(unit, PASSES)
            cols = slice(BANK_ROWS * chunk, BANK_ROWS * (chunk + 1))
            nc.vector.quantize_mx(
                out=wo_codes[:, g, cols].bitcast(FP8X4),
                scales=wo_scales[:, g, cols],
                in_=wo_grouped[unit][:],
            )

        def group_values(g, copy):
            pv_grouped[g] = work.tile(
                [P, K_PASS, 4], BF16, tag="pv_grouped", name="pv_grouped", bufs=1, align_bytes=64
            )
            copy(
                out=pv_grouped[g][:].rearrange("q (c i) j -> q c j i", i=4),
                in_=pv_raw[g][:].rearrange("q j (c i) -> q c j i", i=4),
            )

        def quantise_values(g):
            cols = slice(K_PASS * g, K_PASS * (g + 1))
            nc.vector.quantize_mx(
                out=pv_codes[:, cols].bitcast(FP8X4),
                scales=pv_scales[:, cols],
                in_=pv_grouped[g][:].rearrange("q c j -> q (c j)"),
            )

        def row_max(i):
            r, j = divmod(i, GROUP)
            if j == 0:
                peak[r] = stats.tile([P, GROUP], F32, tag="peak", name="peak")
                shift[r] = stats.tile([P, GROUP], F32, tag="shift", name="shift")
                rowsum[r] = stats.tile([P, GROUP], F32, tag="rowsum", name="rowsum")
            if i >= DFROM:
                nc.vector.tensor_reduce(
                    out=peak[r][:, j : j + 1], in_=banks["score", i][:], axis=mybir.AxisListType.X, op=ALU.max
                )
                nc.gpsimd.tensor_scalar(
                    out=shift[r][:, j : j + 1],
                    in0=peak[r][:, j : j + 1],
                    scalar1=-SCALE,
                    scalar2=0.0,
                    op0=ALU.mult,
                    op1=ALU.add,
                )
                return
            scaled[i] = s_pool.tile([P, PROMPT], F32, tag="scaled", name="scaled")
            nc.vector.tensor_scalar(
                out=scaled[i][:],
                in0=banks["score", i][:],
                scalar1=-SCALE,
                scalar2=None,
                op0=ALU.mult,
                op1=ALU.min,
                accum_out=shift[r][:, j : j + 1],
            )

        def exponential(i):
            r, j = divmod(i, GROUP)
            e_sb[i] = e_pool.tile([P, PROMPT], BF16, tag="e_sb", name="e_sb")
            nc.scalar.activation(
                out=e_sb[i][:],
                in_=banks["score", i][:] if i >= DFROM else scaled[i][:],
                func=ACT.Exp,
                bias=shift[r][:, j : j + 1],
                scale=SCALE if i >= DFROM else -1.0,
                accum_out=rowsum[r][:, j : j + 1],
            )

        def empty_e(pair, copy):
            r, half = divmod(pair, 2)
            if half == 0:
                e_grouped[r] = work.tile(
                    [P, GROUP * P * 4], BF16, tag="e_grouped", name="e_grouped", align_bytes=64
                )
            e_words = e_grouped[r][:].bitcast(F32).rearrange("q (j m u) -> q j m u", j=GROUP, u=2)
            copy(
                out=e_words[:, 2 * half : 2 * half + 2, :, :],
                in_=banks["e", pair][:].rearrange("q j u m -> q j m u"),
            )

        def divide_gate(r):
            g = r % PASSES
            weight[r] = stats.tile([P, GROUP], F32, tag="weight", name="weight")
            nc.gpsimd.tensor_mul(
                out=weight[r][:], in0=rowsum[r][:], in1=inverse_gate[:, GROUP * g : GROUP * (g + 1)]
            )

        def quantise_e(r):
            e_codes[r] = work.tile([P, GROUP * P], U32, tag="e_codes", name="e_codes", align_bytes=64)
            e_scales[r] = work.tile([P, GROUP * P], U8, tag="e_scales", name="e_scales", align_bytes=64)
            nc.vector.quantize_mx(
                out=e_codes[r][:].bitcast(FP8X4), scales=e_scales[r][:], in_=e_grouped[r][:]
            )
            nc.vector.reciprocal(out=weight[r][:], in_=weight[r][:])

        def combine(r, heads):
            rt, g = divmod(r, PASSES)
            b, t = divmod(rt, 2)
            if heads[0] == 0:
                fused[r] = work.tile([P, K_PASS], BF16, tag="fused", name="fused", bufs=4)
            for j in heads:
                nc.vector.scalar_tensor_tensor(
                    out=fused[r][:, HEAD_DIM * j : HEAD_DIM * (j + 1)],
                    in0=num_ps[r][:, j, :],
                    scalar=weight[r][:, j : j + 1],
                    in1=ha_sb[:, b, GROUP * g + j, HEAD_DIM * t : HEAD_DIM * (t + 1)],
                    op0=ALU.mult,
                    op1=ALU.add,
                )

        def empty_fused(r):
            n_rounds = len(fused_rounds(r))
            f_grouped[r] = work.tile(
                [P, n_rounds * P * 4], BF16, tag="f_grouped", name="f_grouped", align_bytes=64
            )
            nc.scalar.copy(
                out=f_grouped[r][:].bitcast(F32).rearrange("q (n m u) -> q n m u", n=n_rounds, u=2),
                in_=banks["fused", r][:].rearrange("q n u m -> q n m u"),
            )

        def quantise_fused(r):
            cols = slice(P * fused_rounds(r)[0], P * (r + 1))
            nc.vector.quantize_mx(
                out=fused_codes[:, cols].bitcast(FP8X4), scales=fused_scales[:, cols], in_=f_grouped[r][:]
            )

        def store(piece, copy):
            rt, n = divmod(piece, N_TILES)
            b, t = divmod(rt, 2)
            result = results.tile([P, N_TILE], F32, tag="result")
            copy(out=result[:], in_=acc[piece][:])
            nc.sync.dma_start(out=out_view[b, t][:, N_TILE * n : N_TILE * (n + 1)], in_=result[:])

        on_vector, on_scalar = nc.vector.tensor_copy, nc.scalar.copy
        ctx.enter_context(tc.manual_schedule())

        load_keys(0, 0, GROUP)
        load_queries(0, 0)
        load_keys(1, 0, GROUP)
        load_queries(0, 1)
        load_values(0)
        nc.sync.dma_start(
            out=gate_bf[:], in_=prompt_gate.rearrange("a h b c -> (a h b c)").partition_broadcast(P)
        )
        load_wo(0)
        load_keys(2, 0, GROUP)
        load_queries(0, 2)
        load_values(1)
        load_keys(3, 0, GROUP)
        load_queries(0, 3)
        load_wo(1)
        load_values(2)
        load_attention(0, 0)
        load_attention(0, 1)
        load_values(3)
        load_attention(0, 2)
        load_attention(0, 3)
        flip_keys(0, 1)
        flip_queries(0, 0, [0])
        flip_keys(1, 1)
        empty_keys(0, 1, on_vector)
        empty_queries(0, 0, [0], on_scalar)
        empty_keys(1, 1, on_vector)
        keys_out, queries_out, wo_out, e_out, f_out, piece_out = None, [], None, [], None, None


        def soon(nominal, earliest):
            return min(nominal, max(STEPS, earliest))

        e_flip, e_quant, values, combines, f_flip, f_quant = {}, {}, {}, {}, {}, {}
        for r in range(ROUNDS):
            E_FLIP, E_QUANT, VALUES, COMBINE, F_FLIP, F_QUANT = LAGS if r < LFROM else LAGS2
            for p in (2 * r, 2 * r + 1):
                fed = soon(2 * p + E_FLIP, 2 * p + 2 + EL)
                e_flip[fed] = e_flip.get(fed, []) + [p]
            fed = soon(GROUP * r + E_QUANT, fed + 2)
            e_quant[fed] = r
            fed = soon(GROUP * r + VALUES, fed + 1)
            values[fed] = r
            fed = soon(GROUP * r + COMBINE, fed)
            combines[fed] = r
            if fused_rounds(r):
                fed = soon(GROUP * r + F_FLIP, fed + 1)
                f_flip[fed] = r
                fed = soon(GROUP * r + F_QUANT, fed + 2)
                f_quant[fed] = r
        fq_step = {r: s for s, r in f_quant.items()}
        key_steps = {KEY_STEP(h): h for h in range(2, HEADS, 2)}
        wo_steps = {wo_unit_step(unit): unit for unit in range(UNITS)}
        wo_quants = {wo_unit_step(u) + WQ: u for u in range(UNITS)}
        project_steps, step = {}, 0
        for rt in range(ROW_TILES - 1):
            for n in range(N_TILES):
                step = max(fq_step[PASSES * rt + PASSES - 1] + 1, wo_unit_step(8 * n + 7) + WQ + 1, step + PEV)
                project_steps[step] = N_TILES * rt + n
        last_quant = fq_step[ROUNDS - 1]
        last_row_tile = {}
        for g in range(PASSES):
            r = ROUNDS - PASSES + g
            s = fq_step.get(r, fq_step.get(r + 1)) + 1
            s = max(s, LPG[g] + last_quant)
            last_row_tile[s] = last_row_tile.get(s, []) + [g]
        for i in range(last_quant + 3):
            if i in (12, 16, 20, 24):
                load_queries(1, i // 4 - 3)
                load_attention(1, i // 4 - 3)
            for load in range(2, 8):
                if i == WO_LOAD(load):
                    load_wo(load)

            if i < STEPS:
                score(i)
            piece = project_steps.get(i)
            if piece is not None and i < STEPS:
                project(piece, range(PASSES))
            pair = e_flip.get(i, [])
            for one in pair:
                flip_e(one)
            r_fused = f_flip.get(i)
            if r_fused is not None:
                flip_fused(r_fused)
            keys = key_steps.get(i)
            if keys is not None:
                flip_keys(keys, 2)
            queries = []
            for b in range(BATCH):
                g = due(i, 2 * HEADS * b - QPH[b], GROUP, PASSES)
                if g is not None:
                    queries.append((b, g, [0, 1]))
            if i == 5:
                queries.append((0, 0, [1]))
            for one in queries:
                flip_queries(*one)
            unit = wo_steps.get(i)
            if unit is not None and not VLAST:
                flip_wo(unit)
            r_values = values.get(i)
            if r_values is not None:
                multiply_values(r_values)
            if unit is not None and VLAST:
                flip_wo(unit)
            if piece is not None and i >= STEPS:
                project(piece, range(PASSES))
            last = last_row_tile.get(i)
            if last:
                for n in range(N_TILES):
                    project(N_TILES * (ROW_TILES - 1) + n, last)

            if i < STEPS and MAXFIRST:
                row_max(i)
            if keys_out is not None and not KEYS_ON_SCALAR(keys_out) and KEYV1:
                empty_keys(keys_out, 2, on_vector)
            g = due(i, PVQ, GROUP, PASSES)
            if g is not None:
                quantise_values(g)
            if i == 5:
                nc.vector.reciprocal(out=inverse_gate[:], in_=gate_bf[:])
            r_e = e_quant.get(i)
            if r_e is not None:
                quantise_e(r_e)
            r_comb = combines.get(i)
            if r_comb is not None:
                combine(r_comb, range(GROUP))
            r_q = f_quant.get(i)
            if r_q is not None:
                quantise_fused(r_q)
            u = wo_quants.get(i)
            if u is not None:
                quantise_wo(u)
            if i < STEPS and not MAXFIRST and not MAXLAST:
                row_max(i)
            if keys_out is not None and not KEYS_ON_SCALAR(keys_out) and not KEYV1:
                empty_keys(keys_out, 2, on_vector)
            for one in queries_out:
                if not Q_ON_SCALAR(one):
                    empty_queries(*one, on_vector)
            if wo_out is not None and WO_ON_VECTOR(wo_out):
                empty_wo(wo_out, on_vector)
            for one in e_out:
                if E_ON_VECTOR(one):
                    empty_e(one, on_vector)
            g = due(i, PVG, GROUP, PASSES)
            if g is not None and not PV_ON_SCALAR(g):
                group_values(g, on_vector)
            if piece_out is not None and OUT_ON_VECTOR(piece_out):
                store(piece_out, on_vector)
            if i < STEPS and MAXLAST:
                row_max(i)

            if EL <= i < STEPS + EL and i >= STEPS - 1:
                exponential(i - EL)
                if (i - EL) % GROUP == GROUP - 1:
                    divide_gate((i - EL) // GROUP)
            for one in e_out:
                if not E_ON_VECTOR(one):
                    empty_e(one, on_scalar)
            if keys_out is not None and KEYS_ON_SCALAR(keys_out):
                empty_keys(keys_out, 2, on_scalar)
            for one in queries_out:
                if Q_ON_SCALAR(one):
                    empty_queries(*one, on_scalar)
            if f_out is not None:
                empty_fused(f_out)
            if i in EARLY:
                exponential(i - 1)
            if EL <= i < STEPS - 1 and i - EL not in [k - 1 for k in EARLY]:
                exponential(i - EL)
                if (i - EL) % GROUP == GROUP - 1:
                    divide_gate((i - EL) // GROUP)
            if wo_out is not None and not WO_ON_VECTOR(wo_out):
                empty_wo(wo_out, on_scalar)
            if g is not None and PV_ON_SCALAR(g):
                group_values(g, on_scalar)
            if piece_out is not None and not OUT_ON_VECTOR(piece_out):
                store(piece_out, on_scalar)
            if i == last_quant + 2:
                for n in range(N_TILES):
                    store(N_TILES * (ROW_TILES - 1) + n, on_vector if n % 2 else on_scalar)
            keys_out, queries_out, wo_out, e_out, f_out, piece_out = keys, queries, unit, pair, r_fused, piece
